import numpy as np
import ml_dtypes


def mxq(x, axis, fmt="e4m3"):
    dtype, down = {"e4m3": (ml_dtypes.float8_e4m3fn, 7), "e5m2": (ml_dtypes.float8_e5m2, 14)}[fmt]
    v = np.moveaxis(np.asarray(x, np.float32).astype(ml_dtypes.bfloat16).astype(np.float64), axis, -1)
    blocks = v.reshape(v.shape[:-1] + (-1, 32))
    amax = np.abs(blocks).max(-1, keepdims=True)
    byte = np.maximum(np.where(amax > 0, np.frexp(amax)[1] - 1 + 127, 0) - down, 1)
    scale = np.exp2(byte - 127.0)
    codes = (blocks / scale).astype(np.float32).astype(dtype).astype(np.float64)
    return np.moveaxis((codes * scale).reshape(v.shape), -1, axis)


WIDE = False


def mx_kscale(k):
    if not WIDE:
        return np.ones(k)
    levels = np.array([10, -10, 5, -5, 0])
    a = np.random.permutation(np.resize(levels, k // 512 * 4)).reshape(k // 512, 4)
    idx = np.arange(k)
    return np.exp2(a[idx // 512, idx % 128 // 32])


BF16 = ml_dtypes.bfloat16


def bf(x):
    return np.asarray(x, np.float32).astype(BF16)


def f64(x):
    return np.asarray(x).astype(np.float64)


T, S, B, E, H = 1024, 128, 8, 1024, 512
SCALE = H ** -0.5


def wn_weight(V, g):
    return V * (g / np.linalg.norm(V, axis=1))[:, None]


def draw_wn(rows, cols, gain, kfac, rfac):
    v0 = np.random.standard_normal((rows, cols)) * np.exp(0.5 * np.random.standard_normal((rows, 1))) * 0.5 / np.sqrt(cols)
    v = bf(v0 / kfac)
    g = gain * (1.0 + 0.1 * np.random.standard_normal(rows)) * rfac * np.linalg.norm(f64(v), axis=1) / np.linalg.norm(v0, axis=1)
    return v, bf(g)


def setup_inputs():
    s, t = mx_kscale(E), mx_kscale(H)
    Vq, gq = draw_wn(H, E, 3.2, s, t)
    Vk, gk = draw_wn(H, E, 0.8, s, 1.0 / t)
    return {"query": bf(np.random.standard_normal((T, B, E)) * s), "key": bf(np.random.standard_normal((S, B, E)) * s),
            "Vq": Vq, "gq": gq, "bq": bf(np.random.standard_normal(H) * 0.4 * t),
            "Vk": Vk, "gk": gk, "bk": bf(np.random.standard_normal(H) * 0.1 / t)}


def reference(query, key, Vq, gq, bq, Vk, gk, bk):
    Wq = wn_weight(f64(Vq), f64(gq))
    Wk = wn_weight(f64(Vk), f64(gk))
    q = ((mxq(f64(query), 2, "e4m3") @ mxq(Wq, 1, "e4m3").T) + f64(bq)) * SCALE
    k = (mxq(f64(key), 2, "e4m3") @ mxq(Wk, 1, "e4m3").T) + f64(bk)
    return mxq(q.transpose(1, 0, 2), 2, "e4m3") @ mxq(k.transpose(1, 2, 0), 1, "e4m3")

@@ -1,0 +1,249 @@
+from contextlib import ExitStack
+
+import concourse.mybir as mybir
+from concourse.masks import make_identity
+
+F32 = mybir.dt.float32
+BF16 = mybir.dt.bfloat16
+U32 = mybir.dt.uint32
+U8 = mybir.dt.uint8
+FP8X4 = mybir.dt.float8_e4m3fn_x4
+ALU = mybir.AluOpType
+ACTF = mybir.ActivationFunctionType
+
+T, S, B, E, H = 1024, 128, 8, 1024, 512
+P = 128
+SCALE = H ** -0.5
+FLOPS = 2 * (T * B * E * H + S * B * E * H + B * T * S * H)
+
+UB = 4
+N_KEY_UNITS = B // UB
+N_UNITS = N_KEY_UNITS + (T // P) * (B // UB)
+AHEAD = 2
+RAW_BUFS = 6
+
+
+def tile_singleheadattention_pa_t_kernel(tc, query, key, Vq, gq, bq, Vk, gk, bk, out):
+    nc = tc.nc
+    with ExitStack() as ctx:
+        const = ctx.enter_context(tc.tile_pool(name="const", bufs=1))
+        rawp = ctx.enter_context(tc.tile_pool(name="rawp", bufs=RAW_BUFS))
+        wgp = ctx.enter_context(tc.tile_pool(name="wgp", bufs=4))
+        xgp = ctx.enter_context(tc.tile_pool(name="xgp", bufs=3))
+        xcp = ctx.enter_context(tc.tile_pool(name="xcp", bufs=4))
+        qgp = ctx.enter_context(tc.tile_pool(name="qgp", bufs=3))
+        qcp = ctx.enter_context(tc.tile_pool(name="qcp", bufs=3))
+        otp = ctx.enter_context(tc.tile_pool(name="otp", bufs=3))
+        ps_t = ctx.enter_context(tc.psum_pool(name="ps_t", bufs=4))
+        ps_q = ctx.enter_context(tc.psum_pool(name="ps_q", bufs=3))
+        ps_l = ctx.enter_context(tc.psum_pool(name="ps_l", bufs=1))
+        ctx.enter_context(tc.manual_schedule())
+
+        vec = {}
+        for nm, src in (("gk", gk), ("gq", gq), ("bk", bk), ("bq", bq)):
+            vt = const.tile([P, 4], BF16, name="vec_" + nm)
+            nc.scalar.dma_start(out=vt[:], in_=src.rearrange("(c j) -> c j", j=4))
+            vec[nm] = vt
+        warm_in = const.tile([P, 1], F32, name="warm_in")
+        warm_out = const.tile([P, 1], F32, name="warm_out")
+        nc.vector.memset(warm_in[:], 1.0)
+        nc.scalar.sqrt(out=warm_out[:], in_=warm_in[:])
+        ident_b = const.tile([P, P], BF16, name="ident_b")
+        ident_f = const.tile([P, P], F32, name="ident_f")
+        make_identity(nc, ident_b[:])
+        make_identity(nc, ident_f[:])
+
+        v_raw, w_sb, ss_a, ss_v, nrm, rnm, s_w, w_c, w_s, bias = {}, {}, {}, {}, {}, {}, {}, {}, {}, {}
+        for w, v_dram in (("k", Vk), ("q", Vq)):
+            v_raw[w] = const.tile([P, 4 * E], BF16, name="v_raw_" + w)
+            nc.sync.dma_start(out=v_raw[w][:], in_=v_dram.rearrange("(c j) e -> c (j e)", j=4))
+            w_sb[w] = const.tile([P, 4 * E], BF16, name="w_sb_" + w)
+            ss_a[w] = const.tile([P, 2], F32, name="ss_a_" + w)
+            ss_v[w] = const.tile([P, 2], F32, name="ss_v_" + w)
+            nrm[w] = const.tile([P, 4], F32, name="nrm_" + w)
+            rnm[w] = const.tile([P, 4], F32, name="rnm_" + w)
+            s_w[w] = const.tile([P, 4], F32, name="s_w_" + w)
+            bias[w] = const.tile([P, 4], F32, name="bias_" + w)
+            w_c[w] = const.tile([P, 4 * 2 * P], U32, name="w_c_" + w, align_bytes=64)
+            w_s[w] = const.tile([P, 4 * 2 * P], U8, name="w_s_" + w, align_bytes=64)
+        junk_a = const.tile([P, E], BF16, name="junk_a")
+        junk_v = const.tile([P, E], F32, name="junk_v")
+        k_c = const.tile([P, B * S], U32, name="k_c", align_bytes=64)
+        k_s = const.tile([P, B * S], U8, name="k_s", align_bytes=64)
+        post_scale = {"k": 1.0, "q": SCALE}
+
+        raw, xg, xc, xs, qg, qc, qs, wg = {}, {}, {}, {}, {}, {}, {}, {}
+
+        def load(u):
+            if u >= N_UNITS:
+                return
+            raw[u] = rawp.tile([P, UB * E], BF16, name="raw")
+            if u < N_KEY_UNITS:
+                src = key[:, UB * u:UB * (u + 1), :]
+            else:
+                c, h = divmod(u - N_KEY_UNITS, B // UB)
+                src = query[P * c:P * (c + 1), UB * h:UB * (h + 1), :]
+            nc.sync.dma_start(out=raw[u][:], in_=src.rearrange("t b e -> t (b e)"))
+
+        def square_act(w, j):
+            nc.scalar.activation(out=junk_a[:], in_=v_raw[w][:, j * E:(j + 1) * E], func=ACTF.Square,
+                                 accum_out=ss_a[w][:, j:j + 1])
+
+        def square_dve(w, j):
+            vj = v_raw[w][:, j * E:(j + 1) * E]
+            nc.vector.scalar_tensor_tensor(out=junk_v[:], in0=vj, scalar=1.0, in1=vj, op0=ALU.mult, op1=ALU.mult,
+                                           accum_out=ss_v[w][:, j - 2:j - 1])
+
+        def row_scale(w):
+            nc.scalar.sqrt(out=nrm[w][:, 0:2], in_=ss_a[w][:])
+            nc.scalar.sqrt(out=nrm[w][:, 2:4], in_=ss_v[w][:])
+            nc.vector.reciprocal(out=rnm[w][:], in_=nrm[w][:])
+            nc.vector.tensor_tensor(out=s_w[w][:], in0=rnm[w][:], in1=vec["g" + w][:], op=ALU.mult)
+
+        def w_mult(w, j):
+            nc.vector.tensor_scalar(out=w_sb[w][:, j * E:(j + 1) * E], in0=v_raw[w][:, j * E:(j + 1) * E],
+                                    scalar1=s_w[w][:, j:j + 1], scalar2=None, op0=ALU.mult)
+
+        def w_transpose(w, j, engine):
+            wv = w_sb[w][:].rearrange("p (j g u c e) -> p j g u e c", j=4, g=2, u=2, e=2)
+            wb = ps_t.tile([P, 8 * P], BF16, name="wb", tag="tb")
+            for g in range(2):
+                for u in range(2):
+                    for e in range(2):
+                        col = (g * 4 + 2 * u + e) * P
+                        nc.tensor.transpose(out=wb[:, col:col + P], in_=wv[:, j, g, u, e, :], identity=ident_b[:])
+            wg[(w, j)] = wgp.tile([P, 8 * P], BF16, name="wg", align_bytes=64)
+            dst = wg[(w, j)][:].rearrange("p (g c t) -> p g c t", g=2, t=4)
+            srcv = wb[:].rearrange("p (g t c) -> p g c t", g=2, t=4)
+            if engine == "act":
+                nc.scalar.copy(out=dst, in_=srcv)
+            else:
+                nc.vector.tensor_copy(out=dst, in_=srcv)
+
+        def w_quant(w, j):
+            cols = slice(j * 2 * P, (j + 1) * 2 * P)
+            nc.vector.quantize_mx(out=w_c[w][:, cols].bitcast(FP8X4), scales=w_s[w][:, cols], in_=wg[(w, j)][:])
+
+        def transposes(u):
+            if u >= N_UNITS:
+                return
+            xg[u] = xgp.tile([P, UB * E], BF16, name="xg", align_bytes=64)
+            src_w = raw[u][:].bitcast(F32)
+            dst_w = xg[u][:].bitcast(F32)
+            for b in range(UB):
+                tb = ps_t.tile([P, 4 * P], F32, name="tb", tag="tb")
+                for gu in range(4):
+                    col = b * 4 * P + gu * P
+                    nc.tensor.transpose(out=tb[:, gu * P:(gu + 1) * P], in_=src_w[:, col:col + P], identity=ident_f[:])
+                nc.scalar.copy(out=dst_w[:, b * 4 * P:(b + 1) * 4 * P].rearrange("p (g r u) -> p g r u", g=2, u=2),
+                               in_=tb[:].rearrange("p (g u r) -> p g r u", g=2, u=2))
+
+        def quant_x(u):
+            if u >= N_UNITS:
+                return
+            xc[u] = xcp.tile([P, UB * 2 * P], U32, name="xc", align_bytes=64)
+            xs[u] = xcp.tile([P, UB * 2 * P], U8, name="xs", align_bytes=64)
+            nc.vector.quantize_mx(out=xc[u][:].bitcast(FP8X4), scales=xs[u][:], in_=xg[u][:])
+
+        def project(u, b):
+            w = "k" if u < N_KEY_UNITS else "q"
+            if b == 0:
+                qg[u] = qgp.tile([P, UB * P * 4], BF16, name="qg", align_bytes=64)
+            qb = ps_q.tile([P, 4 * P], F32, name="qb")
+            for j in range(4):
+                for g in range(2):
+                    wcols = slice((j * 2 + g) * P, (j * 2 + g + 1) * P)
+                    xcols = slice((b * 2 + g) * P, (b * 2 + g + 1) * P)
+                    nc.tensor.matmul_mx(out=qb[:, j * P:(j + 1) * P],
+                                        lhsT=w_c[w][:, wcols].bitcast(FP8X4), lhsT_scale=w_s[w][:, wcols],
+                                        rhs=xc[u][:, xcols].bitcast(FP8X4), rhs_scale=xs[u][:, xcols],
+                                        start=(g == 0), stop=(g == 1))
+            nc.vector.scalar_tensor_tensor(
+                out=qg[u][:, b * 4 * P:(b + 1) * 4 * P].rearrange("p (r j) -> p r j", j=4),
+                in0=qb[:].rearrange("p (j r) -> p r j", j=4), scalar=post_scale[w],
+                in1=bias[w][:].unsqueeze(1).to_broadcast([P, P, 4]), op0=ALU.mult, op1=ALU.add)
+
+        def quant_q(u):
+            if u < 0 or u >= N_UNITS:
+                return
+            if u < N_KEY_UNITS:
+                cols = slice(u * UB * P, (u + 1) * UB * P)
+                nc.vector.quantize_mx(out=k_c[:, cols].bitcast(FP8X4), scales=k_s[:, cols], in_=qg[u][:])
+            else:
+                qc[u] = qcp.tile([P, UB * P], U32, name="qc", align_bytes=64)
+                qs[u] = qcp.tile([P, UB * P], U8, name="qs", align_bytes=64)
+                nc.vector.quantize_mx(out=qc[u][:].bitcast(FP8X4), scales=qs[u][:], in_=qg[u][:])
+
+        def logits(u):
+            if u < N_KEY_UNITS or u >= N_UNITS:
+                return
+            c, h = divmod(u - N_KEY_UNITS, B // UB)
+            lb = ps_l.tile([P, UB * S], F32, name="lb")
+            for i in range(UB):
+                qcols = slice(i * P, (i + 1) * P)
+                kcols = slice((h * UB + i) * S, (h * UB + i + 1) * S)
+                nc.tensor.matmul_mx(out=lb[:, i * S:(i + 1) * S],
+                                    lhsT=qc[u][:, qcols].bitcast(FP8X4), lhsT_scale=qs[u][:, qcols],
+                                    rhs=k_c[:, kcols].bitcast(FP8X4), rhs_scale=k_s[:, kcols],
+                                    start=True, stop=True)
+            ot = otp.tile([P, UB * S], F32, name="ot")
+            nc.scalar.copy(out=ot[:], in_=lb[:])
+            nc.scalar.dma_start(out=out[UB * h:UB * (h + 1), P * c:P * (c + 1), :].rearrange("b t s -> t b s"),
+                                in_=ot[:].rearrange("p (b s) -> p b s", b=UB))
+
+        for u in range(RAW_BUFS):
+            load(u)
+        square_act("k", 0)
+        square_dve("k", 2)
+        square_act("k", 1)
+        square_dve("k", 3)
+        row_scale("k")
+        square_act("q", 0)
+        square_act("q", 1)
+        for j in range(4):
+            w_mult("k", j)
+        nc.vector.tensor_copy(out=bias["k"][:], in_=vec["bk"][:])
+        nc.vector.tensor_scalar(out=bias["q"][:], in0=vec["bq"][:], scalar1=SCALE, scalar2=None, op0=ALU.mult)
+        square_dve("q", 2)
+        w_transpose("k", 0, "act")
+        w_transpose("k", 1, "dve")
+        w_quant("k", 0)
+        w_transpose("k", 2, "act")
+        square_dve("q", 3)
+        w_quant("k", 1)
+        w_transpose("k", 3, "dve")
+        w_quant("k", 2)
+        row_scale("q")
+        transposes(0)
+        load(RAW_BUFS)
+        w_quant("k", 3)
+        for j in range(4):
+            w_mult("q", j)
+        quant_x(0)
+        transposes(1)
+        load(RAW_BUFS + 1)
+        w_transpose("q", 0, "act")
+        quant_x(1)
+        w_transpose("q", 1, "act")
+        w_quant("q", 0)
+        w_transpose("q", 2, "act")
+        w_quant("q", 1)
+        w_transpose("q", 3, "act")
+        w_quant("q", 2)
+        pending_w = [("q", 3)]
+        for i in range(N_UNITS + 1):
+            transposes(i + AHEAD)
+            load(i + AHEAD + RAW_BUFS)
+            if i < N_UNITS:
+                project(i, 0)
+            for wj in pending_w:
+                w_quant(wj[0], wj[1])
+            pending_w = []
+            quant_q(i - 1)
+            if i < N_UNITS:
+                project(i, 1)
+            quant_x(i + AHEAD)
+            if i < N_UNITS:
+                project(i, 2)
+                project(i, 3)
+            logits(i - 1)

@@ -17,10 +17,67 @@ SCALE = H ** -0.5
 FLOPS = 2 * (T * B * E * H + S * B * E * H + B * T * S * H)
 
 UB = 4
-N_KEY_UNITS = B // UB
-N_UNITS = N_KEY_UNITS + (T // P) * (B // UB)
+HALVES = B // UB
+N_X = (T // P) * HALVES
 AHEAD = 2
 RAW_BUFS = 6
+SEQ = [("k", 0), ("k", 1)] + [("q", i) for i in range(N_X)]
+
+
+PLAN = [
+    ('ldv', 'k', 4), ('ldv', 'q', 4), ('ld', 0), ('ld', 1), ('ld', 2), ('ld', 3), ('ld', 4), ('ld', 5),
+    ('bias',), ('sq', 'k', 0, 'act'), ('sq', 'k', 1, 'dve'), ('sq', 'k', 2, 'act'), ('sq', 'k', 3, 'dve'),
+    ('scale', 'k'), ('sq', 'q', 0, 'act'), ('mult', 'k', 0, 'dve'), ('mult', 'k', 1, 'dve'), ('mult', 'k', 2, 'dve'),
+    ('mult', 'k', 3, 'dve'), ('wt', 'k', 0, 0, 'act'), ('wt', 'k', 0, 1, 'dve'), ('wt', 'k', 1, 0, 'act'),
+    ('wt', 'k', 1, 1, 'dve'), ('wq', 'k', 0), ('wt', 'k', 2, 0, 'act'), ('wt', 'k', 2, 1, 'dve'), ('wq', 'k', 1),
+    ('wt', 'k', 3, 0, 'act'), ('wt', 'k', 3, 1, 'dve'), ('wq', 'k', 2), ('sq', 'q', 1, 'dve'), ('T', 0, 0, 'act'),
+    ('T', 0, 1, 'act'), ('sq', 'q', 2, 'act'), ('T', 0, 2, 'act'), ('T', 0, 3, 'act'), ('ld', 6), ('wq', 'k', 3),
+    ('qx', 0, 0), ('qx', 0, 1), ('sq', 'q', 3, 'dve'), ('qx', 0, 2), ('qx', 0, 3), ('T', 1, 0, 'act'),
+    ('T', 1, 1, 'act'), ('T', 1, 2, 'dve'), ('T', 1, 3, 'act'), ('ld', 7), ('scale', 'q'), ('mult', 'q', 0, 'dve'),
+    ('mult', 'q', 1, 'dve'), ('mult', 'q', 2, 'dve'), ('mult', 'q', 3, 'dve'), ('T', 2, 0, 'act'), ('T', 2, 1, 'act'),
+    ('T', 2, 2, 'act'), ('T', 2, 3, 'act'), ('ld', 8), ('P', 0, 0), ('qx', 1, 0), ('qx', 2, 0), ('P', 0, 1),
+    ('qx', 1, 1), ('qx', 2, 1), ('P', 0, 2), ('qx', 1, 2), ('qx', 2, 2), ('qq', 0, 0), ('P', 0, 3), ('qx', 1, 3),
+    ('qx', 2, 3), ('wt', 'q', 0, 0, 'act'), ('wt', 'q', 0, 1, 'act'), ('wt', 'q', 1, 0, 'act'), ('wt', 'q', 1, 1, 'act'),
+    ('wt', 'q', 2, 0, 'act'), ('wt', 'q', 2, 1, 'act'), ('wt', 'q', 3, 0, 'act'), ('wt', 'q', 3, 1, 'act'),
+    ('T', 3, 0, 'act'), ('T', 3, 1, 'act'), ('T', 3, 2, 'act'), ('T', 3, 3, 'act'), ('ld', 9), ('wq', 'q', 0),
+    ('wq', 'q', 1), ('wq', 'q', 2), ('wq', 'q', 3), ('P', 1, 0), ('qx', 3, 0), ('qq', 0, 1), ('P', 1, 1),
+    ('qx', 3, 1), ('P', 1, 2), ('qx', 3, 2), ('qq', 1, 0), ('P', 1, 3), ('qx', 3, 3), ('T', 4, 0, 'act'),
+    ('T', 4, 1, 'act'), ('T', 4, 2, 'act'), ('T', 4, 3, 'act'), ('ld', 10), ('P', 2, 0), ('qx', 4, 0),
+    ('qq', 1, 1), ('P', 2, 1), ('qx', 4, 1), ('P', 2, 2), ('qx', 4, 2), ('qq', 2, 0), ('P', 2, 3), ('qx', 4, 3),
+    ('T', 5, 0, 'act'), ('T', 5, 1, 'act'), ('T', 5, 2, 'act'), ('T', 5, 3, 'act'), ('ld', 11), ('P', 3, 0),
+    ('qx', 5, 0), ('qq', 2, 1), ('P', 3, 1), ('qx', 5, 1), ('P', 3, 2), ('qx', 5, 2), ('qq', 3, 0), ('P', 3, 3),
+    ('qx', 5, 3), ('L', 2), ('T', 6, 0, 'act'), ('T', 6, 1, 'act'), ('T', 6, 2, 'act'), ('T', 6, 3, 'act'),
+    ('ld', 12), ('P', 4, 0), ('qx', 6, 0), ('qq', 3, 1), ('P', 4, 1), ('qx', 6, 1), ('P', 4, 2), ('qx', 6, 2),
+    ('qq', 4, 0), ('P', 4, 3), ('qx', 6, 3), ('L', 3), ('T', 7, 0, 'act'), ('T', 7, 1, 'act'), ('T', 7, 2, 'act'),
+    ('T', 7, 3, 'act'), ('ld', 13), ('P', 5, 0), ('qx', 7, 0), ('qq', 4, 1), ('P', 5, 1), ('qx', 7, 1),
+    ('P', 5, 2), ('qx', 7, 2), ('qq', 5, 0), ('P', 5, 3), ('qx', 7, 3), ('L', 4), ('T', 8, 0, 'act'),
+    ('T', 8, 1, 'act'), ('T', 8, 2, 'act'), ('T', 8, 3, 'act'), ('ld', 14), ('P', 6, 0), ('qx', 8, 0),
+    ('qq', 5, 1), ('P', 6, 1), ('qx', 8, 1), ('P', 6, 2), ('qx', 8, 2), ('qq', 6, 0), ('P', 6, 3), ('qx', 8, 3),
+    ('L', 5), ('T', 9, 0, 'act'), ('T', 9, 1, 'act'), ('T', 9, 2, 'act'), ('T', 9, 3, 'act'), ('ld', 15),
+    ('P', 7, 0), ('qx', 9, 0), ('qq', 6, 1), ('P', 7, 1), ('qx', 9, 1), ('P', 7, 2), ('qx', 9, 2), ('qq', 7, 0),
+    ('P', 7, 3), ('qx', 9, 3), ('L', 6), ('T', 10, 0, 'act'), ('T', 10, 1, 'act'), ('T', 10, 2, 'act'),
+    ('T', 10, 3, 'act'), ('ld', 16), ('P', 8, 0), ('qx', 10, 0), ('qq', 7, 1), ('P', 8, 1), ('qx', 10, 1),
+    ('P', 8, 2), ('qx', 10, 2), ('qq', 8, 0), ('P', 8, 3), ('qx', 10, 3), ('L', 7), ('T', 11, 0, 'act'),
+    ('T', 11, 1, 'act'), ('T', 11, 2, 'act'), ('T', 11, 3, 'act'), ('ld', 17), ('P', 9, 0), ('qx', 11, 0),
+    ('qq', 8, 1), ('P', 9, 1), ('qx', 11, 1), ('P', 9, 2), ('qx', 11, 2), ('qq', 9, 0), ('P', 9, 3), ('qx', 11, 3),
+    ('L', 8), ('T', 12, 0, 'act'), ('T', 12, 1, 'act'), ('T', 12, 2, 'act'), ('T', 12, 3, 'act'), ('P', 10, 0),
+    ('qx', 12, 0), ('qq', 9, 1), ('P', 10, 1), ('qx', 12, 1), ('P', 10, 2), ('qx', 12, 2), ('qq', 10, 0),
+    ('P', 10, 3), ('qx', 12, 3), ('L', 9), ('T', 13, 0, 'act'), ('T', 13, 1, 'act'), ('T', 13, 2, 'act'),
+    ('T', 13, 3, 'act'), ('P', 11, 0), ('qx', 13, 0), ('qq', 10, 1), ('P', 11, 1), ('qx', 13, 1), ('P', 11, 2),
+    ('qx', 13, 2), ('qq', 11, 0), ('P', 11, 3), ('qx', 13, 3), ('L', 10), ('T', 14, 0, 'act'), ('T', 14, 1, 'act'),
+    ('T', 14, 2, 'act'), ('T', 14, 3, 'act'), ('P', 12, 0), ('qx', 14, 0), ('qq', 11, 1), ('P', 12, 1),
+    ('qx', 14, 1), ('P', 12, 2), ('qx', 14, 2), ('qq', 12, 0), ('P', 12, 3), ('qx', 14, 3), ('L', 11),
+    ('T', 15, 0, 'act'), ('T', 15, 1, 'act'), ('T', 15, 2, 'act'), ('T', 15, 3, 'act'), ('P', 13, 0),
+    ('qx', 15, 0), ('qq', 12, 1), ('P', 13, 1), ('qx', 15, 1), ('P', 13, 2), ('qx', 15, 2), ('qq', 13, 0),
+    ('P', 13, 3), ('qx', 15, 3), ('L', 12), ('T', 16, 0, 'act'), ('T', 16, 1, 'act'), ('T', 16, 2, 'act'),
+    ('T', 16, 3, 'act'), ('P', 14, 0), ('qx', 16, 0), ('qq', 13, 1), ('P', 14, 1), ('qx', 16, 1), ('P', 14, 2),
+    ('qx', 16, 2), ('qq', 14, 0), ('P', 14, 3), ('qx', 16, 3), ('L', 13), ('T', 17, 0, 'act'), ('T', 17, 1, 'act'),
+    ('T', 17, 2, 'act'), ('T', 17, 3, 'act'), ('P', 15, 0), ('qx', 17, 0), ('qq', 14, 1), ('P', 15, 1),
+    ('qx', 17, 1), ('P', 15, 2), ('qx', 17, 2), ('qq', 15, 0), ('P', 15, 3), ('qx', 17, 3), ('L', 14),
+    ('P', 16, 0), ('qq', 15, 1), ('P', 16, 1), ('P', 16, 2), ('qq', 16, 0), ('P', 16, 3), ('L', 15), ('P', 17, 0),
+    ('qq', 16, 1), ('P', 17, 1), ('P', 17, 2), ('qq', 17, 0), ('P', 17, 3), ('L', 16), ('qq', 17, 1),
+    ('L', 17),
+]
 
 
 def tile_singleheadattention_pa_t_kernel(tc, query, key, Vq, gq, bq, Vk, gk, bk, out):
@@ -28,7 +85,7 @@ def tile_singleheadattention_pa_t_kernel(tc, query, key, Vq, gq, bq, Vk, gk, bk,
     with ExitStack() as ctx:
         const = ctx.enter_context(tc.tile_pool(name="const", bufs=1))
         rawp = ctx.enter_context(tc.tile_pool(name="rawp", bufs=RAW_BUFS))
-        wgp = ctx.enter_context(tc.tile_pool(name="wgp", bufs=4))
+        wgp = ctx.enter_context(tc.tile_pool(name="wgp", bufs=3))
         xgp = ctx.enter_context(tc.tile_pool(name="xgp", bufs=3))
         xcp = ctx.enter_context(tc.tile_pool(name="xcp", bufs=4))
         qgp = ctx.enter_context(tc.tile_pool(name="qgp", bufs=3))
@@ -40,7 +97,7 @@ def tile_singleheadattention_pa_t_kernel(tc, query, key, Vq, gq, bq, Vk, gk, bk,
         ctx.enter_context(tc.manual_schedule())
 
         vec = {}
-        for nm, src in (("gk", gk), ("gq", gq), ("bk", bk), ("bq", bq)):
+        for nm, src in (("gq", gq), ("bq", bq), ("gk", gk), ("bk", bk)):
             vt = const.tile([P, 4], BF16, name="vec_" + nm)
             nc.scalar.dma_start(out=vt[:], in_=src.rearrange("(c j) -> c j", j=4))
             vec[nm] = vt
@@ -48,18 +105,17 @@ def tile_singleheadattention_pa_t_kernel(tc, query, key, Vq, gq, bq, Vk, gk, bk,
         warm_out = const.tile([P, 1], F32, name="warm_out")
         nc.vector.memset(warm_in[:], 1.0)
         nc.scalar.sqrt(out=warm_out[:], in_=warm_in[:])
-        ident_b = const.tile([P, P], BF16, name="ident_b")
         ident_f = const.tile([P, P], F32, name="ident_f")
-        make_identity(nc, ident_b[:])
+        ident_b = const.tile([P, P], BF16, name="ident_b")
         make_identity(nc, ident_f[:])
+        make_identity(nc, ident_b[:])
 
         v_raw, w_sb, ss_a, ss_v, nrm, rnm, s_w, w_c, w_s, bias = {}, {}, {}, {}, {}, {}, {}, {}, {}, {}
-        for w, v_dram in (("k", Vk), ("q", Vq)):
+        for w in ("q", "k"):
             v_raw[w] = const.tile([P, 4 * E], BF16, name="v_raw_" + w)
-            nc.sync.dma_start(out=v_raw[w][:], in_=v_dram.rearrange("(c j) e -> c (j e)", j=4))
             w_sb[w] = const.tile([P, 4 * E], BF16, name="w_sb_" + w)
-            ss_a[w] = const.tile([P, 2], F32, name="ss_a_" + w)
-            ss_v[w] = const.tile([P, 2], F32, name="ss_v_" + w)
+            ss_a[w] = const.tile([P, 4], F32, name="ss_a_" + w)
+            ss_v[w] = const.tile([P, 4], F32, name="ss_v_" + w)
             nrm[w] = const.tile([P, 4], F32, name="nrm_" + w)
             rnm[w] = const.tile([P, 4], F32, name="rnm_" + w)
             s_w[w] = const.tile([P, 4], F32, name="s_w_" + w)
@@ -71,50 +127,64 @@ def tile_singleheadattention_pa_t_kernel(tc, query, key, Vq, gq, bq, Vk, gk, bk,
         k_c = const.tile([P, B * S], U32, name="k_c", align_bytes=64)
         k_s = const.tile([P, B * S], U8, name="k_s", align_bytes=64)
         post_scale = {"k": 1.0, "q": SCALE}
+        v_dram = {"q": Vq, "k": Vk}
 
         raw, xg, xc, xs, qg, qc, qs, wg = {}, {}, {}, {}, {}, {}, {}, {}
 
-        def load(u):
-            if u >= N_UNITS:
+        def load_v(w, pieces):
+            src = v_dram[w].rearrange("(c j) e -> c j e", j=4)
+            step = 4 // pieces
+            for i in range(pieces):
+                nc.sync.dma_start(out=v_raw[w][:, i * step * E:(i + 1) * step * E].rearrange("c (j e) -> c j e", j=step),
+                                  in_=src[:, i * step:(i + 1) * step, :])
+
+        def load(n):
+            if n >= len(SEQ):
                 return
+            u = SEQ[n]
             raw[u] = rawp.tile([P, UB * E], BF16, name="raw")
-            if u < N_KEY_UNITS:
-                src = key[:, UB * u:UB * (u + 1), :]
+            if u[0] == "k":
+                src = key[:, UB * u[1]:UB * (u[1] + 1), :]
             else:
-                c, h = divmod(u - N_KEY_UNITS, B // UB)
+                c, h = divmod(u[1], HALVES)
                 src = query[P * c:P * (c + 1), UB * h:UB * (h + 1), :]
             nc.sync.dma_start(out=raw[u][:], in_=src.rearrange("t b e -> t (b e)"))
 
-        def square_act(w, j):
-            nc.scalar.activation(out=junk_a[:], in_=v_raw[w][:, j * E:(j + 1) * E], func=ACTF.Square,
-                                 accum_out=ss_a[w][:, j:j + 1])
-
-        def square_dve(w, j):
+        def square(w, j, engine):
             vj = v_raw[w][:, j * E:(j + 1) * E]
-            nc.vector.scalar_tensor_tensor(out=junk_v[:], in0=vj, scalar=1.0, in1=vj, op0=ALU.mult, op1=ALU.mult,
-                                           accum_out=ss_v[w][:, j - 2:j - 1])
+            if engine == "act":
+                nc.scalar.activation(out=junk_a[:], in_=vj, func=ACTF.Square, accum_out=ss_a[w][:, j:j + 1])
+            else:
+                nc.vector.scalar_tensor_tensor(out=junk_v[:], in0=vj, scalar=1.0, in1=vj, op0=ALU.mult, op1=ALU.mult,
+                                               accum_out=ss_v[w][:, j:j + 1])
 
-        def row_scale(w):
-            nc.scalar.sqrt(out=nrm[w][:, 0:2], in_=ss_a[w][:])
-            nc.scalar.sqrt(out=nrm[w][:, 2:4], in_=ss_v[w][:])
+        def row_scale(w, act_cols, dve_cols):
+            if act_cols is not None:
+                nc.scalar.sqrt(out=nrm[w][:, act_cols], in_=ss_a[w][:, act_cols])
+            if dve_cols is not None:
+                nc.scalar.sqrt(out=nrm[w][:, dve_cols], in_=ss_v[w][:, dve_cols])
             nc.vector.reciprocal(out=rnm[w][:], in_=nrm[w][:])
             nc.vector.tensor_tensor(out=s_w[w][:], in0=rnm[w][:], in1=vec["g" + w][:], op=ALU.mult)
 
-        def w_mult(w, j):
-            nc.vector.tensor_scalar(out=w_sb[w][:, j * E:(j + 1) * E], in0=v_raw[w][:, j * E:(j + 1) * E],
-                                    scalar1=s_w[w][:, j:j + 1], scalar2=None, op0=ALU.mult)
+        def w_mult(w, j, engine):
+            cols = slice(j * E, (j + 1) * E)
+            if engine == "act":
+                nc.scalar.activation(out=w_sb[w][:, cols], in_=v_raw[w][:, cols], func=ACTF.Copy, scale=s_w[w][:, j:j + 1])
+            else:
+                nc.vector.tensor_scalar(out=w_sb[w][:, cols], in0=v_raw[w][:, cols],
+                                        scalar1=s_w[w][:, j:j + 1], scalar2=None, op0=ALU.mult)
 
-        def w_transpose(w, j, engine):
+        def w_transpose(w, j, g, engine):
             wv = w_sb[w][:].rearrange("p (j g u c e) -> p j g u e c", j=4, g=2, u=2, e=2)
-            wb = ps_t.tile([P, 8 * P], BF16, name="wb", tag="tb")
-            for g in range(2):
-                for u in range(2):
-                    for e in range(2):
-                        col = (g * 4 + 2 * u + e) * P
-                        nc.tensor.transpose(out=wb[:, col:col + P], in_=wv[:, j, g, u, e, :], identity=ident_b[:])
-            wg[(w, j)] = wgp.tile([P, 8 * P], BF16, name="wg", align_bytes=64)
-            dst = wg[(w, j)][:].rearrange("p (g c t) -> p g c t", g=2, t=4)
-            srcv = wb[:].rearrange("p (g t c) -> p g c t", g=2, t=4)
+            wb = ps_t.tile([P, 4 * P], BF16, name="wb", tag="tb")
+            for u in range(2):
+                for e in range(2):
+                    col = (2 * u + e) * P
+                    nc.tensor.transpose(out=wb[:, col:col + P], in_=wv[:, j, g, u, e, :], identity=ident_b[:])
+            if g == 0:
+                wg[(w, j)] = wgp.tile([P, 8 * P], BF16, name="wg", align_bytes=64)
+            dst = wg[(w, j)][:, g * 4 * P:(g + 1) * 4 * P].rearrange("p (c t) -> p c t", t=4)
+            srcv = wb[:].rearrange("p (t c) -> p c t", t=4)
             if engine == "act":
                 nc.scalar.copy(out=dst, in_=srcv)
             else:
@@ -124,31 +194,42 @@ def tile_singleheadattention_pa_t_kernel(tc, query, key, Vq, gq, bq, Vk, gk, bk,
             cols = slice(j * 2 * P, (j + 1) * 2 * P)
             nc.vector.quantize_mx(out=w_c[w][:, cols].bitcast(FP8X4), scales=w_s[w][:, cols], in_=wg[(w, j)][:])
 
-        def transposes(u):
-            if u >= N_UNITS:
+        def transposes(n, b, engine):
+            if n >= len(SEQ):
                 return
-            xg[u] = xgp.tile([P, UB * E], BF16, name="xg", align_bytes=64)
+            u = SEQ[n]
+            if b == 0:
+                xg[u] = xgp.tile([P, UB * E], BF16, name="xg", align_bytes=64)
+                xc[u] = xcp.tile([P, UB * 2 * P], U32, name="xc", align_bytes=64)
+                xs[u] = xcp.tile([P, UB * 2 * P], U8, name="xs", align_bytes=64)
             src_w = raw[u][:].bitcast(F32)
             dst_w = xg[u][:].bitcast(F32)
-            for b in range(UB):
-                tb = ps_t.tile([P, 4 * P], F32, name="tb", tag="tb")
-                for gu in range(4):
-                    col = b * 4 * P + gu * P
-                    nc.tensor.transpose(out=tb[:, gu * P:(gu + 1) * P], in_=src_w[:, col:col + P], identity=ident_f[:])
-                nc.scalar.copy(out=dst_w[:, b * 4 * P:(b + 1) * 4 * P].rearrange("p (g r u) -> p g r u", g=2, u=2),
-                               in_=tb[:].rearrange("p (g u r) -> p g r u", g=2, u=2))
+            tb = ps_t.tile([P, 4 * P], F32, name="tb", tag="tb")
+            for gu in range(4):
+                col = b * 4 * P + gu * P
+                nc.tensor.transpose(out=tb[:, gu * P:(gu + 1) * P], in_=src_w[:, col:col + P], identity=ident_f[:])
+            dst = dst_w[:, b * 4 * P:(b + 1) * 4 * P].rearrange("p (g r u) -> p g r u", g=2, u=2)
+            srcv = tb[:].rearrange("p (g u r) -> p g r u", g=2, u=2)
+            if engine == "act":
+                nc.scalar.copy(out=dst, in_=srcv)
+            else:
+                nc.vector.tensor_copy(out=dst, in_=srcv)
 
-        def quant_x(u):
-            if u >= N_UNITS:
+        def quant_x(n, b):
+            if n >= len(SEQ):
                 return
-            xc[u] = xcp.tile([P, UB * 2 * P], U32, name="xc", align_bytes=64)
-            xs[u] = xcp.tile([P, UB * 2 * P], U8, name="xs", align_bytes=64)
-            nc.vector.quantize_mx(out=xc[u][:].bitcast(FP8X4), scales=xs[u][:], in_=xg[u][:])
+            u = SEQ[n]
+            cols = slice(b * 2 * P, (b + 1) * 2 * P)
+            nc.vector.quantize_mx(out=xc[u][:, cols].bitcast(FP8X4), scales=xs[u][:, cols],
+                                  in_=xg[u][:, b * E:(b + 1) * E])
 
         def project(u, b):
-            w = "k" if u < N_KEY_UNITS else "q"
+            w = u[0]
             if b == 0:
                 qg[u] = qgp.tile([P, UB * P * 4], BF16, name="qg", align_bytes=64)
+                if w == "q":
+                    qc[u] = qcp.tile([P, UB * P], U32, name="qc", align_bytes=64)
+                    qs[u] = qcp.tile([P, UB * P], U8, name="qs", align_bytes=64)
             qb = ps_q.tile([P, 4 * P], F32, name="qb")
             for j in range(4):
                 for g in range(2):
@@ -163,21 +244,17 @@ def tile_singleheadattention_pa_t_kernel(tc, query, key, Vq, gq, bq, Vk, gk, bk,
                 in0=qb[:].rearrange("p (j r) -> p r j", j=4), scalar=post_scale[w],
                 in1=bias[w][:].unsqueeze(1).to_broadcast([P, P, 4]), op0=ALU.mult, op1=ALU.add)
 
-        def quant_q(u):
-            if u < 0 or u >= N_UNITS:
-                return
-            if u < N_KEY_UNITS:
-                cols = slice(u * UB * P, (u + 1) * UB * P)
-                nc.vector.quantize_mx(out=k_c[:, cols].bitcast(FP8X4), scales=k_s[:, cols], in_=qg[u][:])
+        def quant_q(u, b0, nb):
+            src = qg[u][:, b0 * 4 * P:(b0 + nb) * 4 * P]
+            if u[0] == "k":
+                cols = slice((u[1] * UB + b0) * P, (u[1] * UB + b0 + nb) * P)
+                nc.vector.quantize_mx(out=k_c[:, cols].bitcast(FP8X4), scales=k_s[:, cols], in_=src)
             else:
-                qc[u] = qcp.tile([P, UB * P], U32, name="qc", align_bytes=64)
-                qs[u] = qcp.tile([P, UB * P], U8, name="qs", align_bytes=64)
-                nc.vector.quantize_mx(out=qc[u][:].bitcast(FP8X4), scales=qs[u][:], in_=qg[u][:])
+                cols = slice(b0 * P, (b0 + nb) * P)
+                nc.vector.quantize_mx(out=qc[u][:, cols].bitcast(FP8X4), scales=qs[u][:, cols], in_=src)
 
         def logits(u):
-            if u < N_KEY_UNITS or u >= N_UNITS:
-                return
-            c, h = divmod(u - N_KEY_UNITS, B // UB)
+            c, h = divmod(u[1], HALVES)
             lb = ps_l.tile([P, UB * S], F32, name="lb")
             for i in range(UB):
                 qcols = slice(i * P, (i + 1) * P)
@@ -191,59 +268,15 @@ def tile_singleheadattention_pa_t_kernel(tc, query, key, Vq, gq, bq, Vk, gk, bk,
             nc.scalar.dma_start(out=out[UB * h:UB * (h + 1), P * c:P * (c + 1), :].rearrange("b t s -> t b s"),
                                 in_=ot[:].rearrange("p (b s) -> p b s", b=UB))
 
-        for u in range(RAW_BUFS):
-            load(u)
-        square_act("k", 0)
-        square_dve("k", 2)
-        square_act("k", 1)
-        square_dve("k", 3)
-        row_scale("k")
-        square_act("q", 0)
-        square_act("q", 1)
-        for j in range(4):
-            w_mult("k", j)
-        nc.vector.tensor_copy(out=bias["k"][:], in_=vec["bk"][:])
-        nc.vector.tensor_scalar(out=bias["q"][:], in0=vec["bq"][:], scalar1=SCALE, scalar2=None, op0=ALU.mult)
-        square_dve("q", 2)
-        w_transpose("k", 0, "act")
-        w_transpose("k", 1, "dve")
-        w_quant("k", 0)
-        w_transpose("k", 2, "act")
-        square_dve("q", 3)
-        w_quant("k", 1)
-        w_transpose("k", 3, "dve")
-        w_quant("k", 2)
-        row_scale("q")
-        transposes(0)
-        load(RAW_BUFS)
-        w_quant("k", 3)
-        for j in range(4):
-            w_mult("q", j)
-        quant_x(0)
-        transposes(1)
-        load(RAW_BUFS + 1)
-        w_transpose("q", 0, "act")
-        quant_x(1)
-        w_transpose("q", 1, "act")
-        w_quant("q", 0)
-        w_transpose("q", 2, "act")
-        w_quant("q", 1)
-        w_transpose("q", 3, "act")
-        w_quant("q", 2)
-        pending_w = [("q", 3)]
-        for i in range(N_UNITS + 1):
-            transposes(i + AHEAD)
-            load(i + AHEAD + RAW_BUFS)
-            if i < N_UNITS:
-                project(i, 0)
-            for wj in pending_w:
-                w_quant(wj[0], wj[1])
-            pending_w = []
-            quant_q(i - 1)
-            if i < N_UNITS:
-                project(i, 1)
-            quant_x(i + AHEAD)
-            if i < N_UNITS:
-                project(i, 2)
-                project(i, 3)
-            logits(i - 1)
+        def bias_prep():
+            nc.vector.tensor_copy(out=bias["k"][:], in_=vec["bk"][:])
+            nc.vector.tensor_scalar(out=bias["q"][:], in0=vec["bq"][:], scalar1=SCALE, scalar2=None, op0=ALU.mult)
+
+        do = {
+            "ldv": load_v, "ld": load, "sq": square, "mult": w_mult, "wt": w_transpose, "wq": w_quant,
+            "scale": lambda w: row_scale(w, slice(0, 4, 2), slice(1, 4, 2)), "bias": bias_prep,
+            "T": transposes, "qx": quant_x, "P": lambda n, b: project(SEQ[n], b),
+            "qq": lambda n, h: quant_q(SEQ[n], 2 * h, 2), "L": lambda n: logits(SEQ[n]),
+        }
+        for step in PLAN:
+            do[step[0]](*step[1:])

@@ -27,27 +27,27 @@ SEQ = [("k", 0), ("k", 1)] + [("q", i) for i in range(N_X)]
 PLAN = [
     ('ldv', 'k', 4), ('ldv', 'q', 4), ('ld', 0), ('ld', 1), ('ld', 2), ('ld', 3), ('ld', 4), ('ld', 5),
     ('bias',), ('sq', 'k', 0, 'act'), ('sq', 'k', 1, 'dve'), ('sq', 'k', 2, 'act'), ('sq', 'k', 3, 'dve'),
-    ('scale', 'k'), ('sq', 'q', 0, 'act'), ('mult', 'k', 0, 'dve'), ('mult', 'k', 1, 'dve'), ('mult', 'k', 2, 'dve'),
-    ('mult', 'k', 3, 'dve'), ('wt', 'k', 0, 0, 'act'), ('wt', 'k', 0, 1, 'dve'), ('wt', 'k', 1, 0, 'act'),
-    ('wt', 'k', 1, 1, 'dve'), ('wq', 'k', 0), ('wt', 'k', 2, 0, 'act'), ('wt', 'k', 2, 1, 'dve'), ('wq', 'k', 1),
-    ('wt', 'k', 3, 0, 'act'), ('wt', 'k', 3, 1, 'dve'), ('wq', 'k', 2), ('sq', 'q', 1, 'dve'), ('T', 0, 0, 'act'),
-    ('T', 0, 1, 'act'), ('sq', 'q', 2, 'act'), ('T', 0, 2, 'act'), ('T', 0, 3, 'act'), ('ld', 6), ('wq', 'k', 3),
-    ('qx', 0, 0), ('qx', 0, 1), ('sq', 'q', 3, 'dve'), ('qx', 0, 2), ('qx', 0, 3), ('T', 1, 0, 'act'),
-    ('T', 1, 1, 'act'), ('T', 1, 2, 'dve'), ('T', 1, 3, 'act'), ('ld', 7), ('scale', 'q'), ('mult', 'q', 0, 'dve'),
-    ('mult', 'q', 1, 'dve'), ('mult', 'q', 2, 'dve'), ('mult', 'q', 3, 'dve'), ('T', 2, 0, 'act'), ('T', 2, 1, 'act'),
-    ('T', 2, 2, 'act'), ('T', 2, 3, 'act'), ('ld', 8), ('P', 0, 0), ('qx', 1, 0), ('qx', 2, 0), ('P', 0, 1),
-    ('qx', 1, 1), ('qx', 2, 1), ('P', 0, 2), ('qx', 1, 2), ('qx', 2, 2), ('qq', 0, 0), ('P', 0, 3), ('qx', 1, 3),
-    ('qx', 2, 3), ('wt', 'q', 0, 0, 'act'), ('wt', 'q', 0, 1, 'act'), ('wt', 'q', 1, 0, 'act'), ('wt', 'q', 1, 1, 'act'),
-    ('wt', 'q', 2, 0, 'act'), ('wt', 'q', 2, 1, 'act'), ('wt', 'q', 3, 0, 'act'), ('wt', 'q', 3, 1, 'act'),
-    ('T', 3, 0, 'act'), ('T', 3, 1, 'act'), ('T', 3, 2, 'act'), ('T', 3, 3, 'act'), ('ld', 9), ('wq', 'q', 0),
-    ('wq', 'q', 1), ('wq', 'q', 2), ('wq', 'q', 3), ('P', 1, 0), ('qx', 3, 0), ('qq', 0, 1), ('P', 1, 1),
-    ('qx', 3, 1), ('P', 1, 2), ('qx', 3, 2), ('qq', 1, 0), ('P', 1, 3), ('qx', 3, 3), ('T', 4, 0, 'act'),
-    ('T', 4, 1, 'act'), ('T', 4, 2, 'act'), ('T', 4, 3, 'act'), ('ld', 10), ('P', 2, 0), ('qx', 4, 0),
-    ('qq', 1, 1), ('P', 2, 1), ('qx', 4, 1), ('P', 2, 2), ('qx', 4, 2), ('qq', 2, 0), ('P', 2, 3), ('qx', 4, 3),
-    ('T', 5, 0, 'act'), ('T', 5, 1, 'act'), ('T', 5, 2, 'act'), ('T', 5, 3, 'act'), ('ld', 11), ('P', 3, 0),
-    ('qx', 5, 0), ('qq', 2, 1), ('P', 3, 1), ('qx', 5, 1), ('P', 3, 2), ('qx', 5, 2), ('qq', 3, 0), ('P', 3, 3),
-    ('qx', 5, 3), ('L', 2), ('T', 6, 0, 'act'), ('T', 6, 1, 'act'), ('T', 6, 2, 'act'), ('T', 6, 3, 'act'),
-    ('ld', 12), ('P', 4, 0), ('qx', 6, 0), ('qq', 3, 1), ('P', 4, 1), ('qx', 6, 1), ('P', 4, 2), ('qx', 6, 2),
+    ('scale', 'k'), ('mult', 'k', 0, 'dve'), ('mult', 'k', 2, 'dve'), ('mult', 'k', 3, 'dve'), ('mult', 'k', 1, 'dve'),
+    ('wt', 'k', 0, 0, 'dve'), ('sq', 'q', 0, 'act'), ('wt', 'k', 0, 1, 'act'), ('wt', 'k', 2, 0, 'act'),
+    ('wq', 'k', 0), ('sq', 'q', 3, 'dve'), ('wt', 'k', 1, 0, 'act'), ('wt', 'k', 3, 0, 'act'), ('sq', 'q', 1, 'dve'),
+    ('T', 0, 0, 'act'), ('T', 0, 1, 'act'), ('wt', 'k', 1, 1, 'dve'), ('sq', 'q', 2, 'act'), ('wt', 'k', 3, 1, 'dve'),
+    ('T', 0, 2, 'act'), ('wq', 'k', 1), ('wt', 'k', 2, 1, 'dve'), ('qx', 0, 0), ('T', 0, 3, 'act'), ('qx', 0, 2),
+    ('T', 1, 0, 'act'), ('T', 1, 1, 'act'), ('wq', 'k', 2), ('wq', 'k', 3), ('T', 1, 2, 'dve'), ('T', 1, 3, 'act'),
+    ('ld', 6), ('qx', 0, 1), ('P', 0, 0), ('scale', 'q'), ('mult', 'q', 2, 'dve'), ('T', 2, 0, 'act'),
+    ('qx', 0, 3), ('T', 2, 1, 'act'), ('mult', 'q', 0, 'dve'), ('mult', 'q', 3, 'dve'), ('qx', 1, 3),
+    ('T', 2, 2, 'act'), ('T', 2, 3, 'dve'), ('ld', 7), ('P', 0, 1), ('qq', 0, 0), ('qx', 2, 3), ('P', 0, 2),
+    ('qx', 1, 0), ('ld', 8), ('mult', 'q', 1, 'act'), ('wt', 'q', 2, 0, 'act'), ('qx', 2, 0), ('wt', 'q', 0, 0, 'act'),
+    ('wt', 'q', 0, 1, 'act'), ('P', 0, 3), ('wt', 'q', 3, 0, 'act'), ('wt', 'q', 1, 0, 'act'), ('wt', 'q', 1, 1, 'act'),
+    ('qx', 1, 2), ('qx', 2, 1), ('wt', 'q', 2, 1, 'act'), ('qx', 1, 1), ('P', 1, 0), ('wq', 'q', 1), ('T', 3, 0, 'act'),
+    ('wq', 'q', 2), ('wq', 'q', 0), ('wt', 'q', 3, 1, 'act'), ('P', 1, 1), ('wq', 'q', 3), ('P', 1, 2),
+    ('qx', 2, 2), ('T', 3, 1, 'act'), ('qq', 0, 1), ('T', 3, 2, 'act'), ('T', 3, 3, 'act'), ('P', 2, 0),
+    ('P', 2, 1), ('ld', 9), ('qq', 1, 0), ('T', 4, 0, 'act'), ('qx', 3, 2), ('T', 4, 1, 'act'), ('T', 4, 2, 'act'),
+    ('T', 4, 3, 'act'), ('qq', 2, 0), ('qx', 3, 1), ('qx', 3, 0), ('P', 1, 3), ('P', 2, 2), ('P', 3, 0),
+    ('qx', 4, 0), ('T', 5, 0, 'act'), ('T', 5, 1, 'act'), ('qx', 4, 1), ('qx', 5, 0), ('qx', 4, 2), ('T', 5, 2, 'act'),
+    ('T', 5, 3, 'act'), ('ld', 10), ('qx', 3, 3), ('qx', 5, 1), ('P', 2, 3), ('P', 3, 1), ('qq', 2, 1),
+    ('P', 3, 2), ('qx', 5, 3), ('qq', 1, 1), ('ld', 11), ('P', 3, 3), ('T', 6, 0, 'act'), ('qx', 4, 3),
+    ('T', 6, 1, 'act'), ('qq', 3, 0), ('T', 6, 2, 'act'), ('T', 6, 3, 'act'), ('ld', 12), ('P', 4, 0),
+    ('L', 2), ('qx', 5, 2), ('qx', 6, 0), ('qq', 3, 1), ('P', 4, 1), ('qx', 6, 1), ('P', 4, 2), ('qx', 6, 2),
     ('qq', 4, 0), ('P', 4, 3), ('qx', 6, 3), ('L', 3), ('T', 7, 0, 'act'), ('T', 7, 1, 'act'), ('T', 7, 2, 'act'),
     ('T', 7, 3, 'act'), ('ld', 13), ('P', 5, 0), ('qx', 7, 0), ('qq', 4, 1), ('P', 5, 1), ('qx', 7, 1),
     ('P', 5, 2), ('qx', 7, 2), ('qq', 5, 0), ('P', 5, 3), ('qx', 7, 3), ('L', 4), ('T', 8, 0, 'act'),
@@ -85,7 +85,7 @@ def tile_singleheadattention_pa_t_kernel(tc, query, key, Vq, gq, bq, Vk, gk, bk,
     with ExitStack() as ctx:
         const = ctx.enter_context(tc.tile_pool(name="const", bufs=1))
         rawp = ctx.enter_context(tc.tile_pool(name="rawp", bufs=RAW_BUFS))
-        wgp = ctx.enter_context(tc.tile_pool(name="wgp", bufs=3))
+        wgp = ctx.enter_context(tc.tile_pool(name="wgp", bufs=4))
         xgp = ctx.enter_context(tc.tile_pool(name="xgp", bufs=3))
         xcp = ctx.enter_context(tc.tile_pool(name="xcp", bufs=4))
         qgp = ctx.enter_context(tc.tile_pool(name="qgp", bufs=3))
@@ -272,7 +272,13 @@ def tile_singleheadattention_pa_t_kernel(tc, query, key, Vq, gq, bq, Vk, gk, bk,
             nc.vector.tensor_copy(out=bias["k"][:], in_=vec["bk"][:])
             nc.vector.tensor_scalar(out=bias["q"][:], in0=vec["bq"][:], scalar1=SCALE, scalar2=None, op0=ALU.mult)
 
+        def warm(count, width):
+            dm = ps_l.tile([P, width], F32, name="dm", tag="lb")
+            for rep in range(count):
+                nc.tensor.matmul(out=dm[:], lhsT=ident_b[:], rhs=v_raw["k"][:, 0:width], start=True, stop=True)
+
         do = {
+            "dm": warm,
             "ldv": load_v, "ld": load, "sq": square, "mult": w_mult, "wt": w_transpose, "wq": w_quant,
             "scale": lambda w: row_scale(w, slice(0, 4, 2), slice(1, 4, 2)), "bias": bias_prep,
             "T": transposes, "qx": quant_x, "P": lambda n, b: project(SEQ[n], b),

@@ -13,70 +13,40 @@ ACTF = mybir.ActivationFunctionType
 
 T, S, B, E, H = 1024, 128, 8, 1024, 512
 P = 128
+PACK = 4
+PASSES = E // (P * PACK)
 SCALE = H ** -0.5
 FLOPS = 2 * (T * B * E * H + S * B * E * H + B * T * S * H)
 
 UB = 4
 HALVES = B // UB
-N_X = (T // P) * HALVES
+UNITS = [("k", h) for h in range(HALVES)] + [("q", i) for i in range((T // P) * HALVES)]
+FIRST_QUERY = HALVES
 AHEAD = 2
 RAW_BUFS = 6
-SEQ = [("k", 0), ("k", 1)] + [("q", i) for i in range(N_X)]
 
-
-PLAN = [
-    ('ldv', 'k', 4), ('ldv', 'q', 4), ('ld', 0), ('ld', 1), ('ld', 2), ('ld', 3), ('ld', 4), ('ld', 5),
-    ('bias',), ('sq', 'k', 0, 'act'), ('sq', 'k', 1, 'dve'), ('sq', 'k', 2, 'act'), ('sq', 'k', 3, 'dve'),
-    ('scale', 'k'), ('mult', 'k', 0, 'dve'), ('mult', 'k', 2, 'dve'), ('mult', 'k', 3, 'dve'), ('mult', 'k', 1, 'dve'),
-    ('wt', 'k', 0, 0, 'dve'), ('sq', 'q', 0, 'act'), ('wt', 'k', 0, 1, 'act'), ('wt', 'k', 2, 0, 'act'),
-    ('wq', 'k', 0), ('sq', 'q', 3, 'dve'), ('wt', 'k', 1, 0, 'act'), ('wt', 'k', 3, 0, 'act'), ('sq', 'q', 1, 'dve'),
-    ('T', 0, 0, 'act'), ('T', 0, 1, 'act'), ('wt', 'k', 1, 1, 'dve'), ('sq', 'q', 2, 'act'), ('wt', 'k', 3, 1, 'dve'),
-    ('T', 0, 2, 'act'), ('wq', 'k', 1), ('wt', 'k', 2, 1, 'dve'), ('qx', 0, 0), ('T', 0, 3, 'act'), ('qx', 0, 2),
-    ('T', 1, 0, 'act'), ('T', 1, 1, 'act'), ('wq', 'k', 2), ('wq', 'k', 3), ('T', 1, 2, 'dve'), ('T', 1, 3, 'act'),
-    ('ld', 6), ('qx', 0, 1), ('P', 0, 0), ('scale', 'q'), ('mult', 'q', 2, 'dve'), ('T', 2, 0, 'act'),
-    ('qx', 0, 3), ('T', 2, 1, 'act'), ('mult', 'q', 0, 'dve'), ('mult', 'q', 3, 'dve'), ('qx', 1, 3),
-    ('T', 2, 2, 'act'), ('T', 2, 3, 'dve'), ('ld', 7), ('P', 0, 1), ('qq', 0, 0), ('qx', 2, 3), ('P', 0, 2),
-    ('qx', 1, 0), ('ld', 8), ('mult', 'q', 1, 'act'), ('wt', 'q', 2, 0, 'act'), ('qx', 2, 0), ('wt', 'q', 0, 0, 'act'),
-    ('wt', 'q', 0, 1, 'act'), ('P', 0, 3), ('wt', 'q', 3, 0, 'act'), ('wt', 'q', 1, 0, 'act'), ('wt', 'q', 1, 1, 'act'),
-    ('qx', 1, 2), ('qx', 2, 1), ('wt', 'q', 2, 1, 'act'), ('qx', 1, 1), ('P', 1, 0), ('wq', 'q', 1), ('T', 3, 0, 'act'),
-    ('wq', 'q', 2), ('wq', 'q', 0), ('wt', 'q', 3, 1, 'act'), ('P', 1, 1), ('wq', 'q', 3), ('P', 1, 2),
-    ('qx', 2, 2), ('T', 3, 1, 'act'), ('qq', 0, 1), ('T', 3, 2, 'act'), ('T', 3, 3, 'act'), ('P', 2, 0),
-    ('P', 2, 1), ('ld', 9), ('qq', 1, 0), ('T', 4, 0, 'act'), ('qx', 3, 2), ('T', 4, 1, 'act'), ('T', 4, 2, 'act'),
-    ('T', 4, 3, 'act'), ('qq', 2, 0), ('qx', 3, 1), ('qx', 3, 0), ('P', 1, 3), ('P', 2, 2), ('P', 3, 0),
-    ('qx', 4, 0), ('T', 5, 0, 'act'), ('T', 5, 1, 'act'), ('qx', 4, 1), ('qx', 5, 0), ('qx', 4, 2), ('T', 5, 2, 'act'),
-    ('T', 5, 3, 'act'), ('ld', 10), ('qx', 3, 3), ('qx', 5, 1), ('P', 2, 3), ('P', 3, 1), ('qq', 2, 1),
-    ('P', 3, 2), ('qx', 5, 3), ('qq', 1, 1), ('ld', 11), ('P', 3, 3), ('T', 6, 0, 'act'), ('qx', 4, 3),
-    ('T', 6, 1, 'act'), ('qq', 3, 0), ('T', 6, 2, 'act'), ('T', 6, 3, 'act'), ('ld', 12), ('P', 4, 0),
-    ('L', 2), ('qx', 5, 2), ('qx', 6, 0), ('qq', 3, 1), ('P', 4, 1), ('qx', 6, 1), ('P', 4, 2), ('qx', 6, 2),
-    ('qq', 4, 0), ('P', 4, 3), ('qx', 6, 3), ('L', 3), ('T', 7, 0, 'act'), ('T', 7, 1, 'act'), ('T', 7, 2, 'act'),
-    ('T', 7, 3, 'act'), ('ld', 13), ('P', 5, 0), ('qx', 7, 0), ('qq', 4, 1), ('P', 5, 1), ('qx', 7, 1),
-    ('P', 5, 2), ('qx', 7, 2), ('qq', 5, 0), ('P', 5, 3), ('qx', 7, 3), ('L', 4), ('T', 8, 0, 'act'),
-    ('T', 8, 1, 'act'), ('T', 8, 2, 'act'), ('T', 8, 3, 'act'), ('ld', 14), ('P', 6, 0), ('qx', 8, 0),
-    ('qq', 5, 1), ('P', 6, 1), ('qx', 8, 1), ('P', 6, 2), ('qx', 8, 2), ('qq', 6, 0), ('P', 6, 3), ('qx', 8, 3),
-    ('L', 5), ('T', 9, 0, 'act'), ('T', 9, 1, 'act'), ('T', 9, 2, 'act'), ('T', 9, 3, 'act'), ('ld', 15),
-    ('P', 7, 0), ('qx', 9, 0), ('qq', 6, 1), ('P', 7, 1), ('qx', 9, 1), ('P', 7, 2), ('qx', 9, 2), ('qq', 7, 0),
-    ('P', 7, 3), ('qx', 9, 3), ('L', 6), ('T', 10, 0, 'act'), ('T', 10, 1, 'act'), ('T', 10, 2, 'act'),
-    ('T', 10, 3, 'act'), ('ld', 16), ('P', 8, 0), ('qx', 10, 0), ('qq', 7, 1), ('P', 8, 1), ('qx', 10, 1),
-    ('P', 8, 2), ('qx', 10, 2), ('qq', 8, 0), ('P', 8, 3), ('qx', 10, 3), ('L', 7), ('T', 11, 0, 'act'),
-    ('T', 11, 1, 'act'), ('T', 11, 2, 'act'), ('T', 11, 3, 'act'), ('ld', 17), ('P', 9, 0), ('qx', 11, 0),
-    ('qq', 8, 1), ('P', 9, 1), ('qx', 11, 1), ('P', 9, 2), ('qx', 11, 2), ('qq', 9, 0), ('P', 9, 3), ('qx', 11, 3),
-    ('L', 8), ('T', 12, 0, 'act'), ('T', 12, 1, 'act'), ('T', 12, 2, 'act'), ('T', 12, 3, 'act'), ('P', 10, 0),
-    ('qx', 12, 0), ('qq', 9, 1), ('P', 10, 1), ('qx', 12, 1), ('P', 10, 2), ('qx', 12, 2), ('qq', 10, 0),
-    ('P', 10, 3), ('qx', 12, 3), ('L', 9), ('T', 13, 0, 'act'), ('T', 13, 1, 'act'), ('T', 13, 2, 'act'),
-    ('T', 13, 3, 'act'), ('P', 11, 0), ('qx', 13, 0), ('qq', 10, 1), ('P', 11, 1), ('qx', 13, 1), ('P', 11, 2),
-    ('qx', 13, 2), ('qq', 11, 0), ('P', 11, 3), ('qx', 13, 3), ('L', 10), ('T', 14, 0, 'act'), ('T', 14, 1, 'act'),
-    ('T', 14, 2, 'act'), ('T', 14, 3, 'act'), ('P', 12, 0), ('qx', 14, 0), ('qq', 11, 1), ('P', 12, 1),
-    ('qx', 14, 1), ('P', 12, 2), ('qx', 14, 2), ('qq', 12, 0), ('P', 12, 3), ('qx', 14, 3), ('L', 11),
-    ('T', 15, 0, 'act'), ('T', 15, 1, 'act'), ('T', 15, 2, 'act'), ('T', 15, 3, 'act'), ('P', 13, 0),
-    ('qx', 15, 0), ('qq', 12, 1), ('P', 13, 1), ('qx', 15, 1), ('P', 13, 2), ('qx', 15, 2), ('qq', 13, 0),
-    ('P', 13, 3), ('qx', 15, 3), ('L', 12), ('T', 16, 0, 'act'), ('T', 16, 1, 'act'), ('T', 16, 2, 'act'),
-    ('T', 16, 3, 'act'), ('P', 14, 0), ('qx', 16, 0), ('qq', 13, 1), ('P', 14, 1), ('qx', 16, 1), ('P', 14, 2),
-    ('qx', 16, 2), ('qq', 14, 0), ('P', 14, 3), ('qx', 16, 3), ('L', 13), ('T', 17, 0, 'act'), ('T', 17, 1, 'act'),
-    ('T', 17, 2, 'act'), ('T', 17, 3, 'act'), ('P', 15, 0), ('qx', 17, 0), ('qq', 14, 1), ('P', 15, 1),
-    ('qx', 17, 1), ('P', 15, 2), ('qx', 17, 2), ('qq', 15, 0), ('P', 15, 3), ('qx', 17, 3), ('L', 14),
-    ('P', 16, 0), ('qq', 15, 1), ('P', 16, 1), ('P', 16, 2), ('qq', 16, 0), ('P', 16, 3), ('L', 15), ('P', 17, 0),
-    ('qq', 16, 1), ('P', 17, 1), ('P', 17, 2), ('qq', 17, 0), ('P', 17, 3), ('L', 16), ('qq', 17, 1),
-    ('L', 17),
+START = [
+    ("load_v", "k"), ("load_v", "q"), ("load", 0), ("load", 1), ("load", 2), ("load", 3), ("load", 4),
+    ("load", 5), ("square", "k", 0, "act"), ("square", "k", 1, "dve"), ("square", "k", 2, "act"),
+    ("square", "k", 3, "dve"), ("scale", "k"), ("square", "q", 0, "act"), ("mult", "k", 0, "dve"),
+    ("mult", "k", 1, "dve"), ("w_t", "k", 0, 0, "act"), ("mult", "k", 2, "dve"), ("mult", "k", 3, "dve"),
+    ("w_t", "k", 0, 1, "dve"), ("w_t", "k", 1, 0, "act"), ("w_t", "k", 1, 1, "dve"), ("w_q", "k", 0),
+    ("w_q", "k", 1), ("w_t", "k", 2, 0, "act"), ("w_t", "k", 2, 1, "act"), ("x_t", 0, 0, "dve"),
+    ("w_t", "k", 3, 0, "act"), ("square", "q", 1, "dve"), ("x_t", 0, 1, "act"), ("x_q", 0, 0),
+    ("x_t", 0, 2, "act"), ("w_t", "k", 3, 1, "dve"), ("x_t", 0, 3, "act"), ("x_t", 1, 0, "act"),
+    ("w_q", "k", 2), ("x_t", 1, 1, "act"), ("square", "q", 2, "act"), ("w_q", "k", 3), ("square", "q", 3, "dve"),
+    ("x_q", 0, 1), ("x_q", 0, 2), ("load", 6), ("bias",), ("x_t", 1, 2, "dve"), ("scale", "q"),
+    ("mult", "q", 0, "dve"), ("x_q", 1, 0), ("proj", 0, 0), ("mult", "q", 1, "dve"), ("x_t", 1, 3, "act"),
+    ("x_t", 2, 0, "act"), ("proj", 0, 1), ("x_q", 2, 0), ("x_t", 2, 1, "act"), ("x_t", 2, 2, "act"),
+    ("w_t", "q", 0, 0, "act"), ("proj", 0, 2), ("w_t", "q", 0, 1, "act"), ("x_q", 0, 3), ("mult", "q", 2, "dve"),
+    ("w_t", "q", 1, 0, "act"), ("q_q", 0, 0), ("x_q", 2, 1), ("w_t", "q", 1, 1, "act"), ("x_q", 2, 2),
+    ("mult", "q", 3, "act"), ("x_q", 1, 1), ("x_t", 2, 3, "act"), ("x_t", 3, 0, "dve"), ("load", 7),
+    ("w_q", "q", 0), ("proj", 0, 3), ("x_t", 3, 1, "act"), ("proj", 1, 0), ("x_q", 1, 2), ("x_q", 1, 3),
+    ("x_t", 3, 2, "act"), ("x_q", 3, 0), ("load", 8), ("q_q", 0, 1), ("w_q", "q", 1), ("w_t", "q", 2, 0, "act"),
+    ("w_t", "q", 2, 1, "act"), ("x_q", 2, 3), ("w_q", "q", 2), ("w_t", "q", 3, 0, "act"), ("w_t", "q", 3, 1, "act"),
+    ("proj", 1, 1), ("proj", 1, 2), ("proj", 1, 3), ("x_t", 3, 3, "act"), ("load", 9), ("w_q", "q", 3),
+    ("x_t", 4, 0, "act"), ("x_t", 4, 1, "act"), ("x_q", 3, 1), ("x_q", 3, 2), ("x_t", 4, 2, "act"),
+    ("x_q", 3, 3), ("q_q", 1, 0), ("x_t", 4, 3, "act"), ("load", 10),
 ]
 
 
@@ -87,7 +57,7 @@ def tile_singleheadattention_pa_t_kernel(tc, query, key, Vq, gq, bq, Vk, gk, bk,
         rawp = ctx.enter_context(tc.tile_pool(name="rawp", bufs=RAW_BUFS))
         wgp = ctx.enter_context(tc.tile_pool(name="wgp", bufs=4))
         xgp = ctx.enter_context(tc.tile_pool(name="xgp", bufs=3))
-        xcp = ctx.enter_context(tc.tile_pool(name="xcp", bufs=4))
+        xcp = ctx.enter_context(tc.tile_pool(name="xcp", bufs=AHEAD + 2))
         qgp = ctx.enter_context(tc.tile_pool(name="qgp", bufs=3))
         qcp = ctx.enter_context(tc.tile_pool(name="qcp", bufs=3))
         otp = ctx.enter_context(tc.tile_pool(name="otp", bufs=3))
@@ -97,192 +67,195 @@ def tile_singleheadattention_pa_t_kernel(tc, query, key, Vq, gq, bq, Vk, gk, bk,
         ctx.enter_context(tc.manual_schedule())
 
         vec = {}
-        for nm, src in (("gq", gq), ("bq", bq), ("gk", gk), ("bk", bk)):
-            vt = const.tile([P, 4], BF16, name="vec_" + nm)
-            nc.scalar.dma_start(out=vt[:], in_=src.rearrange("(c j) -> c j", j=4))
+        for nm, src in (("gk", gk), ("bk", bk), ("gq", gq), ("bq", bq)):
+            vt = const.tile([P, PACK], BF16, name="vec_" + nm)
+            nc.scalar.dma_start(out=vt[:], in_=src.rearrange("(c j) -> c j", j=PACK))
             vec[nm] = vt
         warm_in = const.tile([P, 1], F32, name="warm_in")
         warm_out = const.tile([P, 1], F32, name="warm_out")
         nc.vector.memset(warm_in[:], 1.0)
         nc.scalar.sqrt(out=warm_out[:], in_=warm_in[:])
-        ident_f = const.tile([P, P], F32, name="ident_f")
         ident_b = const.tile([P, P], BF16, name="ident_b")
-        make_identity(nc, ident_f[:])
+        ident_f = const.tile([P, P], F32, name="ident_f")
         make_identity(nc, ident_b[:])
+        make_identity(nc, ident_f[:])
 
-        v_raw, w_sb, ss_a, ss_v, nrm, rnm, s_w, w_c, w_s, bias = {}, {}, {}, {}, {}, {}, {}, {}, {}, {}
-        for w in ("q", "k"):
-            v_raw[w] = const.tile([P, 4 * E], BF16, name="v_raw_" + w)
-            w_sb[w] = const.tile([P, 4 * E], BF16, name="w_sb_" + w)
-            ss_a[w] = const.tile([P, 4], F32, name="ss_a_" + w)
-            ss_v[w] = const.tile([P, 4], F32, name="ss_v_" + w)
-            nrm[w] = const.tile([P, 4], F32, name="nrm_" + w)
-            rnm[w] = const.tile([P, 4], F32, name="rnm_" + w)
-            s_w[w] = const.tile([P, 4], F32, name="s_w_" + w)
-            bias[w] = const.tile([P, 4], F32, name="bias_" + w)
-            w_c[w] = const.tile([P, 4 * 2 * P], U32, name="w_c_" + w, align_bytes=64)
-            w_s[w] = const.tile([P, 4 * 2 * P], U8, name="w_s_" + w, align_bytes=64)
-        junk_a = const.tile([P, E], BF16, name="junk_a")
-        junk_v = const.tile([P, E], F32, name="junk_v")
-        k_c = const.tile([P, B * S], U32, name="k_c", align_bytes=64)
-        k_s = const.tile([P, B * S], U8, name="k_s", align_bytes=64)
-        post_scale = {"k": 1.0, "q": SCALE}
         v_dram = {"q": Vq, "k": Vk}
+        post_scale = {"q": SCALE, "k": 1.0}
+        v_raw, w_sb, ss_act, ss_dve, norm, rnorm, row_gain, w_codes, w_scales, bias = {}, {}, {}, {}, {}, {}, {}, {}, {}, {}
+        for w in ("k", "q"):
+            v_raw[w] = const.tile([P, PACK * E], BF16, name="v_raw_" + w)
+            w_sb[w] = const.tile([P, PACK * E], BF16, name="w_sb_" + w)
+            ss_act[w] = const.tile([P, PACK], F32, name="ss_act_" + w)
+            ss_dve[w] = const.tile([P, PACK], F32, name="ss_dve_" + w)
+            norm[w] = const.tile([P, PACK], F32, name="norm_" + w)
+            rnorm[w] = const.tile([P, PACK], F32, name="rnorm_" + w)
+            row_gain[w] = const.tile([P, PACK], F32, name="row_gain_" + w)
+            bias[w] = const.tile([P, PACK], F32, name="bias_" + w)
+            w_codes[w] = const.tile([P, PACK * PASSES * P], U32, name="w_codes_" + w, align_bytes=64)
+            w_scales[w] = const.tile([P, PACK * PASSES * P], U8, name="w_scales_" + w, align_bytes=64)
+        squares_act = const.tile([P, E], BF16, name="squares_act")
+        squares_dve = const.tile([P, E], F32, name="squares_dve")
+        k_codes = const.tile([P, B * S], U32, name="k_codes", align_bytes=64)
+        k_scales = const.tile([P, B * S], U8, name="k_scales", align_bytes=64)
 
-        raw, xg, xc, xs, qg, qc, qs, wg = {}, {}, {}, {}, {}, {}, {}, {}
+        raw, x_grouped, x_codes, x_scales, q_grouped, q_codes, q_scales, w_grouped = {}, {}, {}, {}, {}, {}, {}, {}
 
-        def load_v(w, pieces):
-            src = v_dram[w].rearrange("(c j) e -> c j e", j=4)
-            step = 4 // pieces
-            for i in range(pieces):
-                nc.sync.dma_start(out=v_raw[w][:, i * step * E:(i + 1) * step * E].rearrange("c (j e) -> c j e", j=step),
-                                  in_=src[:, i * step:(i + 1) * step, :])
+        def load_v(w):
+            src = v_dram[w].rearrange("(c j) e -> c j e", j=PACK)
+            for j in range(PACK):
+                nc.sync.dma_start(out=v_raw[w][:, j * E:(j + 1) * E], in_=src[:, j, :])
 
         def load(n):
-            if n >= len(SEQ):
-                return
-            u = SEQ[n]
-            raw[u] = rawp.tile([P, UB * E], BF16, name="raw")
-            if u[0] == "k":
-                src = key[:, UB * u[1]:UB * (u[1] + 1), :]
+            kind, i = UNITS[n]
+            raw[n] = rawp.tile([P, UB * E], BF16, name="raw")
+            if kind == "k":
+                src = key[:, UB * i:UB * (i + 1), :]
             else:
-                c, h = divmod(u[1], HALVES)
+                c, h = divmod(i, HALVES)
                 src = query[P * c:P * (c + 1), UB * h:UB * (h + 1), :]
-            nc.sync.dma_start(out=raw[u][:], in_=src.rearrange("t b e -> t (b e)"))
+            nc.sync.dma_start(out=raw[n][:], in_=src.rearrange("t b e -> t (b e)"))
 
         def square(w, j, engine):
             vj = v_raw[w][:, j * E:(j + 1) * E]
             if engine == "act":
-                nc.scalar.activation(out=junk_a[:], in_=vj, func=ACTF.Square, accum_out=ss_a[w][:, j:j + 1])
+                nc.scalar.activation(out=squares_act[:], in_=vj, func=ACTF.Square, accum_out=ss_act[w][:, j:j + 1])
             else:
-                nc.vector.scalar_tensor_tensor(out=junk_v[:], in0=vj, scalar=1.0, in1=vj, op0=ALU.mult, op1=ALU.mult,
-                                               accum_out=ss_v[w][:, j:j + 1])
+                nc.vector.scalar_tensor_tensor(out=squares_dve[:], in0=vj, scalar=1.0, in1=vj, op0=ALU.mult,
+                                               op1=ALU.mult, accum_out=ss_dve[w][:, j:j + 1])
 
-        def row_scale(w, act_cols, dve_cols):
-            if act_cols is not None:
-                nc.scalar.sqrt(out=nrm[w][:, act_cols], in_=ss_a[w][:, act_cols])
-            if dve_cols is not None:
-                nc.scalar.sqrt(out=nrm[w][:, dve_cols], in_=ss_v[w][:, dve_cols])
-            nc.vector.reciprocal(out=rnm[w][:], in_=nrm[w][:])
-            nc.vector.tensor_tensor(out=s_w[w][:], in0=rnm[w][:], in1=vec["g" + w][:], op=ALU.mult)
+        def scale(w):
+            even, odd = slice(0, PACK, 2), slice(1, PACK, 2)
+            nc.scalar.sqrt(out=norm[w][:, even], in_=ss_act[w][:, even])
+            nc.scalar.sqrt(out=norm[w][:, odd], in_=ss_dve[w][:, odd])
+            nc.vector.reciprocal(out=rnorm[w][:], in_=norm[w][:])
+            nc.vector.tensor_tensor(out=row_gain[w][:], in0=rnorm[w][:], in1=vec["g" + w][:], op=ALU.mult)
 
-        def w_mult(w, j, engine):
+        def mult(w, j, engine):
             cols = slice(j * E, (j + 1) * E)
             if engine == "act":
-                nc.scalar.activation(out=w_sb[w][:, cols], in_=v_raw[w][:, cols], func=ACTF.Copy, scale=s_w[w][:, j:j + 1])
+                nc.scalar.activation(out=w_sb[w][:, cols], in_=v_raw[w][:, cols], func=ACTF.Copy,
+                                     scale=row_gain[w][:, j:j + 1])
             else:
                 nc.vector.tensor_scalar(out=w_sb[w][:, cols], in0=v_raw[w][:, cols],
-                                        scalar1=s_w[w][:, j:j + 1], scalar2=None, op0=ALU.mult)
+                                        scalar1=row_gain[w][:, j:j + 1], scalar2=None, op0=ALU.mult)
 
-        def w_transpose(w, j, g, engine):
-            wv = w_sb[w][:].rearrange("p (j g u c e) -> p j g u e c", j=4, g=2, u=2, e=2)
-            wb = ps_t.tile([P, 4 * P], BF16, name="wb", tag="tb")
+        def w_t(w, j, g, engine):
+            picked = w_sb[w][:].rearrange("c (j g u p h) -> c j g u h p", j=PACK, g=PASSES, u=2, h=2)
+            bank = ps_t.tile([P, PACK * P], BF16, name="w_bank", tag="t_bank")
             for u in range(2):
-                for e in range(2):
-                    col = (2 * u + e) * P
-                    nc.tensor.transpose(out=wb[:, col:col + P], in_=wv[:, j, g, u, e, :], identity=ident_b[:])
+                for h in range(2):
+                    col = (2 * u + h) * P
+                    nc.tensor.transpose(out=bank[:, col:col + P], in_=picked[:, j, g, u, h, :], identity=ident_b[:])
             if g == 0:
-                wg[(w, j)] = wgp.tile([P, 8 * P], BF16, name="wg", align_bytes=64)
-            dst = wg[(w, j)][:, g * 4 * P:(g + 1) * 4 * P].rearrange("p (c t) -> p c t", t=4)
-            srcv = wb[:].rearrange("p (t c) -> p c t", t=4)
+                w_grouped[(w, j)] = wgp.tile([P, PASSES * P * PACK], BF16, name="w_grouped", align_bytes=64)
+            dst = w_grouped[(w, j)][:, g * P * PACK:(g + 1) * P * PACK].rearrange("p (c t) -> p c t", t=PACK)
+            src = bank[:].rearrange("p (t c) -> p c t", t=PACK)
             if engine == "act":
-                nc.scalar.copy(out=dst, in_=srcv)
+                nc.scalar.copy(out=dst, in_=src)
             else:
-                nc.vector.tensor_copy(out=dst, in_=srcv)
+                nc.vector.tensor_copy(out=dst, in_=src)
 
-        def w_quant(w, j):
-            cols = slice(j * 2 * P, (j + 1) * 2 * P)
-            nc.vector.quantize_mx(out=w_c[w][:, cols].bitcast(FP8X4), scales=w_s[w][:, cols], in_=wg[(w, j)][:])
-
-        def transposes(n, b, engine):
-            if n >= len(SEQ):
-                return
-            u = SEQ[n]
-            if b == 0:
-                xg[u] = xgp.tile([P, UB * E], BF16, name="xg", align_bytes=64)
-                xc[u] = xcp.tile([P, UB * 2 * P], U32, name="xc", align_bytes=64)
-                xs[u] = xcp.tile([P, UB * 2 * P], U8, name="xs", align_bytes=64)
-            src_w = raw[u][:].bitcast(F32)
-            dst_w = xg[u][:].bitcast(F32)
-            tb = ps_t.tile([P, 4 * P], F32, name="tb", tag="tb")
-            for gu in range(4):
-                col = b * 4 * P + gu * P
-                nc.tensor.transpose(out=tb[:, gu * P:(gu + 1) * P], in_=src_w[:, col:col + P], identity=ident_f[:])
-            dst = dst_w[:, b * 4 * P:(b + 1) * 4 * P].rearrange("p (g r u) -> p g r u", g=2, u=2)
-            srcv = tb[:].rearrange("p (g u r) -> p g r u", g=2, u=2)
-            if engine == "act":
-                nc.scalar.copy(out=dst, in_=srcv)
-            else:
-                nc.vector.tensor_copy(out=dst, in_=srcv)
-
-        def quant_x(n, b):
-            if n >= len(SEQ):
-                return
-            u = SEQ[n]
-            cols = slice(b * 2 * P, (b + 1) * 2 * P)
-            nc.vector.quantize_mx(out=xc[u][:, cols].bitcast(FP8X4), scales=xs[u][:, cols],
-                                  in_=xg[u][:, b * E:(b + 1) * E])
-
-        def project(u, b):
-            w = u[0]
-            if b == 0:
-                qg[u] = qgp.tile([P, UB * P * 4], BF16, name="qg", align_bytes=64)
-                if w == "q":
-                    qc[u] = qcp.tile([P, UB * P], U32, name="qc", align_bytes=64)
-                    qs[u] = qcp.tile([P, UB * P], U8, name="qs", align_bytes=64)
-            qb = ps_q.tile([P, 4 * P], F32, name="qb")
-            for j in range(4):
-                for g in range(2):
-                    wcols = slice((j * 2 + g) * P, (j * 2 + g + 1) * P)
-                    xcols = slice((b * 2 + g) * P, (b * 2 + g + 1) * P)
-                    nc.tensor.matmul_mx(out=qb[:, j * P:(j + 1) * P],
-                                        lhsT=w_c[w][:, wcols].bitcast(FP8X4), lhsT_scale=w_s[w][:, wcols],
-                                        rhs=xc[u][:, xcols].bitcast(FP8X4), rhs_scale=xs[u][:, xcols],
-                                        start=(g == 0), stop=(g == 1))
-            nc.vector.scalar_tensor_tensor(
-                out=qg[u][:, b * 4 * P:(b + 1) * 4 * P].rearrange("p (r j) -> p r j", j=4),
-                in0=qb[:].rearrange("p (j r) -> p r j", j=4), scalar=post_scale[w],
-                in1=bias[w][:].unsqueeze(1).to_broadcast([P, P, 4]), op0=ALU.mult, op1=ALU.add)
-
-        def quant_q(u, b0, nb):
-            src = qg[u][:, b0 * 4 * P:(b0 + nb) * 4 * P]
-            if u[0] == "k":
-                cols = slice((u[1] * UB + b0) * P, (u[1] * UB + b0 + nb) * P)
-                nc.vector.quantize_mx(out=k_c[:, cols].bitcast(FP8X4), scales=k_s[:, cols], in_=src)
-            else:
-                cols = slice(b0 * P, (b0 + nb) * P)
-                nc.vector.quantize_mx(out=qc[u][:, cols].bitcast(FP8X4), scales=qs[u][:, cols], in_=src)
-
-        def logits(u):
-            c, h = divmod(u[1], HALVES)
-            lb = ps_l.tile([P, UB * S], F32, name="lb")
-            for i in range(UB):
-                qcols = slice(i * P, (i + 1) * P)
-                kcols = slice((h * UB + i) * S, (h * UB + i + 1) * S)
-                nc.tensor.matmul_mx(out=lb[:, i * S:(i + 1) * S],
-                                    lhsT=qc[u][:, qcols].bitcast(FP8X4), lhsT_scale=qs[u][:, qcols],
-                                    rhs=k_c[:, kcols].bitcast(FP8X4), rhs_scale=k_s[:, kcols],
-                                    start=True, stop=True)
-            ot = otp.tile([P, UB * S], F32, name="ot")
-            nc.scalar.copy(out=ot[:], in_=lb[:])
-            nc.scalar.dma_start(out=out[UB * h:UB * (h + 1), P * c:P * (c + 1), :].rearrange("b t s -> t b s"),
-                                in_=ot[:].rearrange("p (b s) -> p b s", b=UB))
+        def w_q(w, j):
+            cols = slice(j * PASSES * P, (j + 1) * PASSES * P)
+            nc.vector.quantize_mx(out=w_codes[w][:, cols].bitcast(FP8X4), scales=w_scales[w][:, cols],
+                                  in_=w_grouped[(w, j)][:])
 
         def bias_prep():
             nc.vector.tensor_copy(out=bias["k"][:], in_=vec["bk"][:])
             nc.vector.tensor_scalar(out=bias["q"][:], in0=vec["bq"][:], scalar1=SCALE, scalar2=None, op0=ALU.mult)
 
-        def warm(count, width):
-            dm = ps_l.tile([P, width], F32, name="dm", tag="lb")
-            for rep in range(count):
-                nc.tensor.matmul(out=dm[:], lhsT=ident_b[:], rhs=v_raw["k"][:, 0:width], start=True, stop=True)
+        def x_t(n, b, engine):
+            if b == 0:
+                x_grouped[n] = xgp.tile([P, UB * E], BF16, name="x_grouped", align_bytes=64)
+                x_codes[n] = xcp.tile([P, UB * PASSES * P], U32, name="x_codes", align_bytes=64)
+                x_scales[n] = xcp.tile([P, UB * PASSES * P], U8, name="x_scales", align_bytes=64)
+            words_in = raw[n][:].bitcast(F32)
+            words_out = x_grouped[n][:].bitcast(F32)
+            row_words = E // 2
+            bank = ps_t.tile([P, row_words], F32, name="x_bank", tag="t_bank")
+            for gu in range(row_words // P):
+                col = b * row_words + gu * P
+                nc.tensor.transpose(out=bank[:, gu * P:(gu + 1) * P], in_=words_in[:, col:col + P], identity=ident_f[:])
+            dst = words_out[:, b * row_words:(b + 1) * row_words].rearrange("p (g r u) -> p g r u", g=PASSES, u=2)
+            src = bank[:].rearrange("p (g u r) -> p g r u", g=PASSES, u=2)
+            if engine == "act":
+                nc.scalar.copy(out=dst, in_=src)
+            else:
+                nc.vector.tensor_copy(out=dst, in_=src)
 
-        do = {
-            "dm": warm,
-            "ldv": load_v, "ld": load, "sq": square, "mult": w_mult, "wt": w_transpose, "wq": w_quant,
-            "scale": lambda w: row_scale(w, slice(0, 4, 2), slice(1, 4, 2)), "bias": bias_prep,
-            "T": transposes, "qx": quant_x, "P": lambda n, b: project(SEQ[n], b),
-            "qq": lambda n, h: quant_q(SEQ[n], 2 * h, 2), "L": lambda n: logits(SEQ[n]),
-        }
-        for step in PLAN:
-            do[step[0]](*step[1:])
+        def x_q(n, b):
+            cols = slice(b * PASSES * P, (b + 1) * PASSES * P)
+            nc.vector.quantize_mx(out=x_codes[n][:, cols].bitcast(FP8X4), scales=x_scales[n][:, cols],
+                                  in_=x_grouped[n][:, b * E:(b + 1) * E])
+
+        def proj(n, b):
+            w = UNITS[n][0]
+            if b == 0:
+                q_grouped[n] = qgp.tile([P, UB * P * PACK], BF16, name="q_grouped", align_bytes=64)
+                if w == "q":
+                    q_codes[n] = qcp.tile([P, UB * P], U32, name="q_codes", align_bytes=64)
+                    q_scales[n] = qcp.tile([P, UB * P], U8, name="q_scales", align_bytes=64)
+            bank = ps_q.tile([P, PACK * P], F32, name="q_bank")
+            for j in range(PACK):
+                for g in range(PASSES):
+                    wcols = slice((j * PASSES + g) * P, (j * PASSES + g + 1) * P)
+                    xcols = slice((b * PASSES + g) * P, (b * PASSES + g + 1) * P)
+                    nc.tensor.matmul_mx(out=bank[:, j * P:(j + 1) * P],
+                                        lhsT=w_codes[w][:, wcols].bitcast(FP8X4), lhsT_scale=w_scales[w][:, wcols],
+                                        rhs=x_codes[n][:, xcols].bitcast(FP8X4), rhs_scale=x_scales[n][:, xcols],
+                                        start=(g == 0), stop=(g == PASSES - 1))
+            nc.vector.scalar_tensor_tensor(
+                out=q_grouped[n][:, b * P * PACK:(b + 1) * P * PACK].rearrange("c (r j) -> c r j", j=PACK),
+                in0=bank[:].rearrange("c (j r) -> c r j", j=PACK), scalar=post_scale[w],
+                in1=bias[w][:].unsqueeze(1).to_broadcast([P, P, PACK]), op0=ALU.mult, op1=ALU.add)
+
+        def q_q(n, half):
+            w, i = UNITS[n]
+            width = UB // 2 * P
+            src = q_grouped[n][:, half * width * PACK:(half + 1) * width * PACK]
+            if w == "k":
+                cols = slice((i * 2 + half) * width, (i * 2 + half + 1) * width)
+                nc.vector.quantize_mx(out=k_codes[:, cols].bitcast(FP8X4), scales=k_scales[:, cols], in_=src)
+            else:
+                cols = slice(half * width, (half + 1) * width)
+                nc.vector.quantize_mx(out=q_codes[n][:, cols].bitcast(FP8X4), scales=q_scales[n][:, cols], in_=src)
+
+        def logits(n):
+            c, h = divmod(UNITS[n][1], HALVES)
+            bank = ps_l.tile([P, UB * S], F32, name="l_bank")
+            for i in range(UB):
+                qcols = slice(i * P, (i + 1) * P)
+                kcols = slice((h * UB + i) * S, (h * UB + i + 1) * S)
+                nc.tensor.matmul_mx(out=bank[:, i * S:(i + 1) * S],
+                                    lhsT=q_codes[n][:, qcols].bitcast(FP8X4), lhsT_scale=q_scales[n][:, qcols],
+                                    rhs=k_codes[:, kcols].bitcast(FP8X4), rhs_scale=k_scales[:, kcols],
+                                    start=True, stop=True)
+            staged = otp.tile([P, UB * S], F32, name="staged")
+            nc.scalar.copy(out=staged[:], in_=bank[:])
+            nc.scalar.dma_start(out=out[UB * h:UB * (h + 1), P * c:P * (c + 1), :].rearrange("b t s -> t b s"),
+                                in_=staged[:].rearrange("t (b s) -> t b s", b=UB))
+
+        steps = {"load_v": load_v, "load": load, "square": square, "scale": scale, "mult": mult, "w_t": w_t,
+                 "w_q": w_q, "bias": bias_prep, "x_t": x_t, "x_q": x_q, "proj": proj, "q_q": q_q}
+        for step in START:
+            steps[step[0]](*step[1:])
+
+        n_units = len(UNITS)
+        for i in range(FIRST_QUERY, n_units + 1):
+            if FIRST_QUERY < i and i + AHEAD < n_units:
+                for b in range(UB):
+                    x_t(i + AHEAD, b, "act")
+            if FIRST_QUERY < i and i + AHEAD + RAW_BUFS < n_units:
+                load(i + AHEAD + RAW_BUFS)
+            for b in range(UB):
+                if i < n_units:
+                    proj(i, b)
+                if i + AHEAD < n_units:
+                    x_q(i + AHEAD, b)
+                if b == 0:
+                    q_q(i - 1, 1)
+                if b == 2 and i < n_units:
+                    q_q(i, 0)
+            if i - 1 >= FIRST_QUERY:
+                logits(i - 1)

@@ -25,30 +25,6 @@ FIRST_QUERY = HALVES
 AHEAD = 2
 RAW_BUFS = 6
 
-START = [
-    ("load_v", "k"), ("load_v", "q"), ("load", 0), ("load", 1), ("load", 2), ("load", 3), ("load", 4),
-    ("load", 5), ("square", "k", 0, "act"), ("square", "k", 1, "dve"), ("square", "k", 2, "act"),
-    ("square", "k", 3, "dve"), ("scale", "k"), ("square", "q", 0, "act"), ("mult", "k", 0, "dve"),
-    ("mult", "k", 1, "dve"), ("w_t", "k", 0, 0, "act"), ("mult", "k", 2, "dve"), ("mult", "k", 3, "dve"),
-    ("w_t", "k", 0, 1, "dve"), ("w_t", "k", 1, 0, "act"), ("w_t", "k", 1, 1, "dve"), ("w_q", "k", 0),
-    ("w_q", "k", 1), ("w_t", "k", 2, 0, "act"), ("w_t", "k", 2, 1, "act"), ("x_t", 0, 0, "dve"),
-    ("w_t", "k", 3, 0, "act"), ("square", "q", 1, "dve"), ("x_t", 0, 1, "act"), ("x_q", 0, 0),
-    ("x_t", 0, 2, "act"), ("w_t", "k", 3, 1, "dve"), ("x_t", 0, 3, "act"), ("x_t", 1, 0, "act"),
-    ("w_q", "k", 2), ("x_t", 1, 1, "act"), ("square", "q", 2, "act"), ("w_q", "k", 3), ("square", "q", 3, "dve"),
-    ("x_q", 0, 1), ("x_q", 0, 2), ("load", 6), ("bias",), ("x_t", 1, 2, "dve"), ("scale", "q"),
-    ("mult", "q", 0, "dve"), ("x_q", 1, 0), ("proj", 0, 0), ("mult", "q", 1, "dve"), ("x_t", 1, 3, "act"),
-    ("x_t", 2, 0, "act"), ("proj", 0, 1), ("x_q", 2, 0), ("x_t", 2, 1, "act"), ("x_t", 2, 2, "act"),
-    ("w_t", "q", 0, 0, "act"), ("proj", 0, 2), ("w_t", "q", 0, 1, "act"), ("x_q", 0, 3), ("mult", "q", 2, "dve"),
-    ("w_t", "q", 1, 0, "act"), ("q_q", 0, 0), ("x_q", 2, 1), ("w_t", "q", 1, 1, "act"), ("x_q", 2, 2),
-    ("mult", "q", 3, "act"), ("x_q", 1, 1), ("x_t", 2, 3, "act"), ("x_t", 3, 0, "dve"), ("load", 7),
-    ("w_q", "q", 0), ("proj", 0, 3), ("x_t", 3, 1, "act"), ("proj", 1, 0), ("x_q", 1, 2), ("x_q", 1, 3),
-    ("x_t", 3, 2, "act"), ("x_q", 3, 0), ("load", 8), ("q_q", 0, 1), ("w_q", "q", 1), ("w_t", "q", 2, 0, "act"),
-    ("w_t", "q", 2, 1, "act"), ("x_q", 2, 3), ("w_q", "q", 2), ("w_t", "q", 3, 0, "act"), ("w_t", "q", 3, 1, "act"),
-    ("proj", 1, 1), ("proj", 1, 2), ("proj", 1, 3), ("x_t", 3, 3, "act"), ("load", 9), ("w_q", "q", 3),
-    ("x_t", 4, 0, "act"), ("x_t", 4, 1, "act"), ("x_q", 3, 1), ("x_q", 3, 2), ("x_t", 4, 2, "act"),
-    ("x_q", 3, 3), ("q_q", 1, 0), ("x_t", 4, 3, "act"), ("load", 10),
-]
-
 
 def tile_singleheadattention_pa_t_kernel(tc, query, key, Vq, gq, bq, Vk, gk, bk, out):
     nc = tc.nc
@@ -116,9 +92,9 @@ def tile_singleheadattention_pa_t_kernel(tc, query, key, Vq, gq, bq, Vk, gk, bk,
                 src = query[P * c:P * (c + 1), UB * h:UB * (h + 1), :]
             nc.sync.dma_start(out=raw[n][:], in_=src.rearrange("t b e -> t (b e)"))
 
-        def square(w, j, engine):
+        def square(w, j):
             vj = v_raw[w][:, j * E:(j + 1) * E]
-            if engine == "act":
+            if j % 2 == 0:
                 nc.scalar.activation(out=squares_act[:], in_=vj, func=ACTF.Square, accum_out=ss_act[w][:, j:j + 1])
             else:
                 nc.vector.scalar_tensor_tensor(out=squares_dve[:], in0=vj, scalar=1.0, in1=vj, op0=ALU.mult,
@@ -131,14 +107,10 @@ def tile_singleheadattention_pa_t_kernel(tc, query, key, Vq, gq, bq, Vk, gk, bk,
             nc.vector.reciprocal(out=rnorm[w][:], in_=norm[w][:])
             nc.vector.tensor_tensor(out=row_gain[w][:], in0=rnorm[w][:], in1=vec["g" + w][:], op=ALU.mult)
 
-        def mult(w, j, engine):
+        def mult(w, j):
             cols = slice(j * E, (j + 1) * E)
-            if engine == "act":
-                nc.scalar.activation(out=w_sb[w][:, cols], in_=v_raw[w][:, cols], func=ACTF.Copy,
-                                     scale=row_gain[w][:, j:j + 1])
-            else:
-                nc.vector.tensor_scalar(out=w_sb[w][:, cols], in0=v_raw[w][:, cols],
-                                        scalar1=row_gain[w][:, j:j + 1], scalar2=None, op0=ALU.mult)
+            nc.vector.tensor_scalar(out=w_sb[w][:, cols], in0=v_raw[w][:, cols],
+                                    scalar1=row_gain[w][:, j:j + 1], scalar2=None, op0=ALU.mult)
 
         def w_t(w, j, g, engine):
             picked = w_sb[w][:].rearrange("c (j g u p h) -> c j g u h p", j=PACK, g=PASSES, u=2, h=2)
@@ -165,7 +137,7 @@ def tile_singleheadattention_pa_t_kernel(tc, query, key, Vq, gq, bq, Vk, gk, bk,
             nc.vector.tensor_copy(out=bias["k"][:], in_=vec["bk"][:])
             nc.vector.tensor_scalar(out=bias["q"][:], in0=vec["bq"][:], scalar1=SCALE, scalar2=None, op0=ALU.mult)
 
-        def x_t(n, b, engine):
+        def x_t(n, b):
             if b == 0:
                 x_grouped[n] = xgp.tile([P, UB * E], BF16, name="x_grouped", align_bytes=64)
                 x_codes[n] = xcp.tile([P, UB * PASSES * P], U32, name="x_codes", align_bytes=64)
@@ -178,11 +150,7 @@ def tile_singleheadattention_pa_t_kernel(tc, query, key, Vq, gq, bq, Vk, gk, bk,
                 col = b * row_words + gu * P
                 nc.tensor.transpose(out=bank[:, gu * P:(gu + 1) * P], in_=words_in[:, col:col + P], identity=ident_f[:])
             dst = words_out[:, b * row_words:(b + 1) * row_words].rearrange("p (g r u) -> p g r u", g=PASSES, u=2)
-            src = bank[:].rearrange("p (g u r) -> p g r u", g=PASSES, u=2)
-            if engine == "act":
-                nc.scalar.copy(out=dst, in_=src)
-            else:
-                nc.vector.tensor_copy(out=dst, in_=src)
+            nc.scalar.copy(out=dst, in_=bank[:].rearrange("p (g u r) -> p g r u", g=PASSES, u=2))
 
         def x_q(n, b):
             cols = slice(b * PASSES * P, (b + 1) * PASSES * P)
@@ -236,26 +204,86 @@ def tile_singleheadattention_pa_t_kernel(tc, query, key, Vq, gq, bq, Vk, gk, bk,
             nc.scalar.dma_start(out=out[UB * h:UB * (h + 1), P * c:P * (c + 1), :].rearrange("b t s -> t b s"),
                                 in_=staged[:].rearrange("t (b s) -> t b s", b=UB))
 
-        steps = {"load_v": load_v, "load": load, "square": square, "scale": scale, "mult": mult, "w_t": w_t,
-                 "w_q": w_q, "bias": bias_prep, "x_t": x_t, "x_q": x_q, "proj": proj, "q_q": q_q}
-        for step in START:
-            steps[step[0]](*step[1:])
+        def transposes(n):
+            for b in range(UB):
+                x_t(n, b)
+
+        def row_tile(i, b, ahead):
+            if i < n_units:
+                proj(i, b)
+            if i + ahead < n_units:
+                x_q(i + ahead, b)
+            if b == 0 and i > 0:
+                q_q(i - 1, 1)
+            if b == 2 and i < n_units:
+                q_q(i, 0)
+
+        def query_weights(j):
+            w_t("q", j, 0, "act")
+            w_t("q", j, 1, "act")
+            w_q("q", j)
 
         n_units = len(UNITS)
+        load_v("k")
+        load_v("q")
+        for n in range(RAW_BUFS):
+            load(n)
+
+        for j in range(PACK):
+            square("k", j)
+        scale("k")
+        square("q", 0)
+        for j in range(PACK):
+            mult("k", j)
+        bias_prep()
+        for j in range(PACK):
+            w_t("k", j, 0, "act")
+            w_t("k", j, 1, "dve")
+            if j > 0:
+                w_q("k", j - 1)
+            if j % 2 == 1:
+                square("q", j)
+        square("q", 2)
+        w_q("k", PACK - 1)
+
+        for b in range(UB):
+            x_t(0, b)
+            if b > 0:
+                x_q(0, b - 1)
+        load(RAW_BUFS)
+        x_q(0, UB - 1)
+        scale("q")
+        for j in range(PACK):
+            mult("q", j)
+        transposes(1)
+        load(RAW_BUFS + 1)
+
+        row_tile(0, 0, 1)
+        row_tile(0, 1, 1)
+        transposes(2)
+        row_tile(0, 2, 1)
+        row_tile(0, 3, 1)
+        query_weights(0)
+        query_weights(1)
+        load(RAW_BUFS + 2)
+        row_tile(1, 0, 1)
+        row_tile(1, 1, 1)
+        query_weights(2)
+        query_weights(3)
+        row_tile(1, 2, 1)
+        row_tile(1, 3, 1)
+        transposes(3)
+        load(RAW_BUFS + 3)
+
         for i in range(FIRST_QUERY, n_units + 1):
-            if FIRST_QUERY < i and i + AHEAD < n_units:
-                for b in range(UB):
-                    x_t(i + AHEAD, b, "act")
-            if FIRST_QUERY < i and i + AHEAD + RAW_BUFS < n_units:
+            if i + AHEAD < n_units:
+                transposes(i + AHEAD)
+            if i + AHEAD + RAW_BUFS < n_units:
                 load(i + AHEAD + RAW_BUFS)
+            if i == FIRST_QUERY:
+                for b in range(UB):
+                    x_q(i + 1, b)
             for b in range(UB):
-                if i < n_units:
-                    proj(i, b)
-                if i + AHEAD < n_units:
-                    x_q(i + AHEAD, b)
-                if b == 0:
-                    q_q(i - 1, 1)
-                if b == 2 and i < n_units:
-                    q_q(i, 0)
+                row_tile(i, b, AHEAD)
             if i - 1 >= FIRST_QUERY:
                 logits(i - 1)

from contextlib import ExitStack

import concourse.mybir as mybir
from concourse.masks import make_identity

F32 = mybir.dt.float32
BF16 = mybir.dt.bfloat16
U32 = mybir.dt.uint32
U8 = mybir.dt.uint8
FP8X4 = mybir.dt.float8_e4m3fn_x4
ALU = mybir.AluOpType
ACTF = mybir.ActivationFunctionType

T, S, B, E, H = 1024, 128, 8, 1024, 512
P = 128
PACK = 4
PASSES = E // (P * PACK)
SCALE = H ** -0.5
FLOPS = 2 * (T * B * E * H + S * B * E * H + B * T * S * H)

UB = 4
HALVES = B // UB
UNITS = [("k", h) for h in range(HALVES)] + [("q", i) for i in range((T // P) * HALVES)]
FIRST_QUERY = HALVES
AHEAD = 2
RAW_BUFS = 6


def tile_singleheadattention_pa_t_kernel(tc, query, key, Vq, gq, bq, Vk, gk, bk, out):
    nc = tc.nc
    with ExitStack() as ctx:
        const = ctx.enter_context(tc.tile_pool(name="const", bufs=1))
        rawp = ctx.enter_context(tc.tile_pool(name="rawp", bufs=RAW_BUFS))
        wgp = ctx.enter_context(tc.tile_pool(name="wgp", bufs=4))
        xgp = ctx.enter_context(tc.tile_pool(name="xgp", bufs=3))
        xcp = ctx.enter_context(tc.tile_pool(name="xcp", bufs=AHEAD + 2))
        qgp = ctx.enter_context(tc.tile_pool(name="qgp", bufs=3))
        qcp = ctx.enter_context(tc.tile_pool(name="qcp", bufs=3))
        otp = ctx.enter_context(tc.tile_pool(name="otp", bufs=3))
        ps_t = ctx.enter_context(tc.psum_pool(name="ps_t", bufs=4))
        ps_q = ctx.enter_context(tc.psum_pool(name="ps_q", bufs=3))
        ps_l = ctx.enter_context(tc.psum_pool(name="ps_l", bufs=1))
        ctx.enter_context(tc.manual_schedule())

        vec = {}
        for nm, src in (("gk", gk), ("bk", bk), ("gq", gq), ("bq", bq)):
            vt = const.tile([P, PACK], BF16, name="vec_" + nm)
            nc.scalar.dma_start(out=vt[:], in_=src.rearrange("(c j) -> c j", j=PACK))
            vec[nm] = vt
        warm_in = const.tile([P, 1], F32, name="warm_in")
        warm_out = const.tile([P, 1], F32, name="warm_out")
        nc.vector.memset(warm_in[:], 1.0)
        nc.scalar.sqrt(out=warm_out[:], in_=warm_in[:])
        ident_b = const.tile([P, P], BF16, name="ident_b")
        ident_f = const.tile([P, P], F32, name="ident_f")
        make_identity(nc, ident_b[:])
        make_identity(nc, ident_f[:])

        v_dram = {"q": Vq, "k": Vk}
        post_scale = {"q": SCALE, "k": 1.0}
        v_raw, w_sb, ss_act, ss_dve, norm, rnorm, row_gain, w_codes, w_scales, bias = {}, {}, {}, {}, {}, {}, {}, {}, {}, {}
        for w in ("k", "q"):
            v_raw[w] = const.tile([P, PACK * E], BF16, name="v_raw_" + w)
            w_sb[w] = const.tile([P, PACK * E], BF16, name="w_sb_" + w)
            ss_act[w] = const.tile([P, PACK], F32, name="ss_act_" + w)
            ss_dve[w] = const.tile([P, PACK], F32, name="ss_dve_" + w)
            norm[w] = const.tile([P, PACK], F32, name="norm_" + w)
            rnorm[w] = const.tile([P, PACK], F32, name="rnorm_" + w)
            row_gain[w] = const.tile([P, PACK], F32, name="row_gain_" + w)
            bias[w] = const.tile([P, PACK], F32, name="bias_" + w)
            w_codes[w] = const.tile([P, PACK * PASSES * P], U32, name="w_codes_" + w, align_bytes=64)
            w_scales[w] = const.tile([P, PACK * PASSES * P], U8, name="w_scales_" + w, align_bytes=64)
        squares_act = const.tile([P, E], BF16, name="squares_act")
        squares_dve = const.tile([P, E], F32, name="squares_dve")
        k_codes = const.tile([P, B * S], U32, name="k_codes", align_bytes=64)
        k_scales = const.tile([P, B * S], U8, name="k_scales", align_bytes=64)

        raw, x_grouped, x_codes, x_scales, q_grouped, q_codes, q_scales, w_grouped = {}, {}, {}, {}, {}, {}, {}, {}

        def load_v(w):
            src = v_dram[w].rearrange("(c j) e -> c j e", j=PACK)
            for j in range(PACK):
                nc.sync.dma_start(out=v_raw[w][:, j * E:(j + 1) * E], in_=src[:, j, :])

        def load(n):
            kind, i = UNITS[n]
            raw[n] = rawp.tile([P, UB * E], BF16, name="raw")
            if kind == "k":
                src = key[:, UB * i:UB * (i + 1), :]
            else:
                c, h = divmod(i, HALVES)
                src = query[P * c:P * (c + 1), UB * h:UB * (h + 1), :]
            nc.sync.dma_start(out=raw[n][:], in_=src.rearrange("t b e -> t (b e)"))

        def square(w, j):
            vj = v_raw[w][:, j * E:(j + 1) * E]
            if j % 2 == 0:
                nc.scalar.activation(out=squares_act[:], in_=vj, func=ACTF.Square, accum_out=ss_act[w][:, j:j + 1])
            else:
                nc.vector.scalar_tensor_tensor(out=squares_dve[:], in0=vj, scalar=1.0, in1=vj, op0=ALU.mult,
                                               op1=ALU.mult, accum_out=ss_dve[w][:, j:j + 1])

        def scale(w):
            even, odd = slice(0, PACK, 2), slice(1, PACK, 2)
            nc.scalar.sqrt(out=norm[w][:, even], in_=ss_act[w][:, even])
            nc.scalar.sqrt(out=norm[w][:, odd], in_=ss_dve[w][:, odd])
            nc.vector.reciprocal(out=rnorm[w][:], in_=norm[w][:])
            nc.vector.tensor_tensor(out=row_gain[w][:], in0=rnorm[w][:], in1=vec["g" + w][:], op=ALU.mult)

        def mult(w, j):
            cols = slice(j * E, (j + 1) * E)
            nc.vector.tensor_scalar(out=w_sb[w][:, cols], in0=v_raw[w][:, cols],
                                    scalar1=row_gain[w][:, j:j + 1], scalar2=None, op0=ALU.mult)

        def w_t(w, j, g, engine):
            picked = w_sb[w][:].rearrange("c (j g u p h) -> c j g u h p", j=PACK, g=PASSES, u=2, h=2)
            bank = ps_t.tile([P, PACK * P], BF16, name="w_bank", tag="t_bank")
            for u in range(2):
                for h in range(2):
                    col = (2 * u + h) * P
                    nc.tensor.transpose(out=bank[:, col:col + P], in_=picked[:, j, g, u, h, :], identity=ident_b[:])
            if g == 0:
                w_grouped[(w, j)] = wgp.tile([P, PASSES * P * PACK], BF16, name="w_grouped", align_bytes=64)
            dst = w_grouped[(w, j)][:, g * P * PACK:(g + 1) * P * PACK].rearrange("p (c t) -> p c t", t=PACK)
            src = bank[:].rearrange("p (t c) -> p c t", t=PACK)
            if engine == "act":
                nc.scalar.copy(out=dst, in_=src)
            else:
                nc.vector.tensor_copy(out=dst, in_=src)

        def w_q(w, j):
            cols = slice(j * PASSES * P, (j + 1) * PASSES * P)
            nc.vector.quantize_mx(out=w_codes[w][:, cols].bitcast(FP8X4), scales=w_scales[w][:, cols],
                                  in_=w_grouped[(w, j)][:])

        def bias_prep():
            nc.vector.tensor_copy(out=bias["k"][:], in_=vec["bk"][:])
            nc.vector.tensor_scalar(out=bias["q"][:], in0=vec["bq"][:], scalar1=SCALE, scalar2=None, op0=ALU.mult)

        def x_t(n, b):
            if b == 0:
                x_grouped[n] = xgp.tile([P, UB * E], BF16, name="x_grouped", align_bytes=64)
                x_codes[n] = xcp.tile([P, UB * PASSES * P], U32, name="x_codes", align_bytes=64)
                x_scales[n] = xcp.tile([P, UB * PASSES * P], U8, name="x_scales", align_bytes=64)
            words_in = raw[n][:].bitcast(F32)
            words_out = x_grouped[n][:].bitcast(F32)
            row_words = E // 2
            bank = ps_t.tile([P, row_words], F32, name="x_bank", tag="t_bank")
            for gu in range(row_words // P):
                col = b * row_words + gu * P
                nc.tensor.transpose(out=bank[:, gu * P:(gu + 1) * P], in_=words_in[:, col:col + P], identity=ident_f[:])
            dst = words_out[:, b * row_words:(b + 1) * row_words].rearrange("p (g r u) -> p g r u", g=PASSES, u=2)
            nc.scalar.copy(out=dst, in_=bank[:].rearrange("p (g u r) -> p g r u", g=PASSES, u=2))

        def x_q(n, b):
            cols = slice(b * PASSES * P, (b + 1) * PASSES * P)
            nc.vector.quantize_mx(out=x_codes[n][:, cols].bitcast(FP8X4), scales=x_scales[n][:, cols],
                                  in_=x_grouped[n][:, b * E:(b + 1) * E])

        def proj(n, b):
            w = UNITS[n][0]
            if b == 0:
                q_grouped[n] = qgp.tile([P, UB * P * PACK], BF16, name="q_grouped", align_bytes=64)
                if w == "q":
                    q_codes[n] = qcp.tile([P, UB * P], U32, name="q_codes", align_bytes=64)
                    q_scales[n] = qcp.tile([P, UB * P], U8, name="q_scales", align_bytes=64)
            bank = ps_q.tile([P, PACK * P], F32, name="q_bank")
            for j in range(PACK):
                for g in range(PASSES):
                    wcols = slice((j * PASSES + g) * P, (j * PASSES + g + 1) * P)
                    xcols = slice((b * PASSES + g) * P, (b * PASSES + g + 1) * P)
                    nc.tensor.matmul_mx(out=bank[:, j * P:(j + 1) * P],
                                        lhsT=w_codes[w][:, wcols].bitcast(FP8X4), lhsT_scale=w_scales[w][:, wcols],
                                        rhs=x_codes[n][:, xcols].bitcast(FP8X4), rhs_scale=x_scales[n][:, xcols],
                                        start=(g == 0), stop=(g == PASSES - 1))
            nc.vector.scalar_tensor_tensor(
                out=q_grouped[n][:, b * P * PACK:(b + 1) * P * PACK].rearrange("c (r j) -> c r j", j=PACK),
                in0=bank[:].rearrange("c (j r) -> c r j", j=PACK), scalar=post_scale[w],
                in1=bias[w][:].unsqueeze(1).to_broadcast([P, P, PACK]), op0=ALU.mult, op1=ALU.add)

        def q_q(n, half):
            w, i = UNITS[n]
            width = UB // 2 * P
            src = q_grouped[n][:, half * width * PACK:(half + 1) * width * PACK]
            if w == "k":
                cols = slice((i * 2 + half) * width, (i * 2 + half + 1) * width)
                nc.vector.quantize_mx(out=k_codes[:, cols].bitcast(FP8X4), scales=k_scales[:, cols], in_=src)
            else:
                cols = slice(half * width, (half + 1) * width)
                nc.vector.quantize_mx(out=q_codes[n][:, cols].bitcast(FP8X4), scales=q_scales[n][:, cols], in_=src)

        def logits(n):
            c, h = divmod(UNITS[n][1], HALVES)
            bank = ps_l.tile([P, UB * S], F32, name="l_bank")
            for i in range(UB):
                qcols = slice(i * P, (i + 1) * P)
                kcols = slice((h * UB + i) * S, (h * UB + i + 1) * S)
                nc.tensor.matmul_mx(out=bank[:, i * S:(i + 1) * S],
                                    lhsT=q_codes[n][:, qcols].bitcast(FP8X4), lhsT_scale=q_scales[n][:, qcols],
                                    rhs=k_codes[:, kcols].bitcast(FP8X4), rhs_scale=k_scales[:, kcols],
                                    start=True, stop=True)
            staged = otp.tile([P, UB * S], F32, name="staged")
            nc.scalar.copy(out=staged[:], in_=bank[:])
            nc.scalar.dma_start(out=out[UB * h:UB * (h + 1), P * c:P * (c + 1), :].rearrange("b t s -> t b s"),
                                in_=staged[:].rearrange("t (b s) -> t b s", b=UB))

        def transposes(n):
            for b in range(UB):
                x_t(n, b)

        def row_tile(i, b, ahead):
            if i < n_units:
                proj(i, b)
            if i + ahead < n_units:
                x_q(i + ahead, b)
            if b == 0 and i > 0:
                q_q(i - 1, 1)
            if b == 2 and i < n_units:
                q_q(i, 0)

        def query_weights(j):
            w_t("q", j, 0, "act")
            w_t("q", j, 1, "act")
            w_q("q", j)

        n_units = len(UNITS)
        load_v("k")
        load_v("q")
        for n in range(RAW_BUFS):
            load(n)

        for j in range(PACK):
            square("k", j)
        scale("k")
        square("q", 0)
        for j in range(PACK):
            mult("k", j)
        bias_prep()
        for j in range(PACK):
            w_t("k", j, 0, "act")
            w_t("k", j, 1, "dve")
            if j > 0:
                w_q("k", j - 1)
            if j % 2 == 1:
                square("q", j)
        square("q", 2)
        w_q("k", PACK - 1)

        for b in range(UB):
            x_t(0, b)
            if b > 0:
                x_q(0, b - 1)
        load(RAW_BUFS)
        x_q(0, UB - 1)
        scale("q")
        for j in range(PACK):
            mult("q", j)
        transposes(1)
        load(RAW_BUFS + 1)

        row_tile(0, 0, 1)
        row_tile(0, 1, 1)
        transposes(2)
        row_tile(0, 2, 1)
        row_tile(0, 3, 1)
        query_weights(0)
        query_weights(1)
        load(RAW_BUFS + 2)
        row_tile(1, 0, 1)
        row_tile(1, 1, 1)
        query_weights(2)
        query_weights(3)
        row_tile(1, 2, 1)
        row_tile(1, 3, 1)
        transposes(3)
        load(RAW_BUFS + 3)

        for i in range(FIRST_QUERY, n_units + 1):
            if i + AHEAD < n_units:
                transposes(i + AHEAD)
            if i + AHEAD + RAW_BUFS < n_units:
                load(i + AHEAD + RAW_BUFS)
            if i == FIRST_QUERY:
                for b in range(UB):
                    x_q(i + 1, b)
            for b in range(UB):
                row_tile(i, b, AHEAD)
            if i - 1 >= FIRST_QUERY:
                logits(i - 1)
